import numpy as np
import ml_dtypes


def mxq(x, axis, fmt="e4m3"):
    dtype, down = {"e4m3": (ml_dtypes.float8_e4m3fn, 7), "e5m2": (ml_dtypes.float8_e5m2, 14)}[fmt]
    v = np.moveaxis(np.asarray(x, np.float32).astype(ml_dtypes.bfloat16).astype(np.float64), axis, -1)
    blocks = v.reshape(v.shape[:-1] + (-1, 32))
    amax = np.abs(blocks).max(-1, keepdims=True)
    byte = np.maximum(np.where(amax > 0, np.frexp(amax)[1] - 1 + 127, 0) - down, 1)
    scale = np.exp2(byte - 127.0)
    codes = (blocks / scale).astype(np.float32).astype(dtype).astype(np.float64)
    return np.moveaxis((codes * scale).reshape(v.shape), -1, axis)


WIDE = False


def mx_kscale(k):
    if not WIDE:
        return np.ones(k)
    levels = np.array([10, -10, 5, -5, 0])
    a = np.random.permutation(np.resize(levels, k // 512 * 4)).reshape(k // 512, 4)
    idx = np.arange(k)
    return np.exp2(a[idx // 512, idx % 128 // 32])


BF16 = ml_dtypes.bfloat16


def bf(x):
    return np.asarray(x, np.float32).astype(BF16)


def f64(x):
    return np.asarray(x).astype(np.float64)


M, NB, BLK = 8192, 8, 64
K = NB * BLK
EPS = 1e-6


def masks():
    rb = np.repeat(np.arange(NB), BLK)
    cb = np.repeat(np.arange(NB), BLK)
    tree_mask = (rb[:, None] == cb[None, :]).astype(np.float64)
    breeze_mask = (rb[:, None] < cb[None, :]).astype(np.float64)
    return tree_mask, breeze_mask


def setup_inputs():
    r = np.exp2(np.round(np.log2(mx_kscale(K)) / 2))
    s = r * r
    return {"x": bf(np.random.standard_normal((M, K)) * s),
            "x_init": bf(np.random.standard_normal((M, K))),
            "treeWeights": bf(np.sqrt(np.abs(np.random.standard_normal((K, K))) / np.sqrt(K / NB)) / r[:, None]),
            "breezeBiasWeights": bf(np.random.standard_normal((K, K)) / np.sqrt(K) / s[:, None])}


def reference(x, x_init, treeWeights, breezeBiasWeights):
    tree_mask, breeze_mask = masks()
    tw = f64(treeWeights)
    tree_matrix = (tw * tw) * tree_mask
    xq = mxq(f64(x), 1, "e4m3")
    breeze_bias = xq @ mxq(f64(breezeBiasWeights) * breeze_mask, 0, "e4m3")
    h = (xq @ mxq(tree_matrix, 0, "e4m3")) + f64(x_init) + breeze_bias
    tree_bias = np.mean(h, axis=0)
    std = np.std(h, axis=0)
    tree_scale = np.sqrt(1.0 / (std + EPS))
    z = (h - tree_bias) * (tree_scale * tree_scale)
    return 1.0 / (1.0 + np.exp(-z))

@@ -1,0 +1,307 @@
+from contextlib import ExitStack
+
+import concourse.mybir as mybir
+from concourse.masks import make_identity
+
+F32 = mybir.dt.float32
+BF16 = mybir.dt.bfloat16
+U32 = mybir.dt.uint32
+U8 = mybir.dt.uint8
+FP8X4 = mybir.dt.float8_e4m3fn_x4
+ALU = mybir.AluOpType
+ACT = mybir.ActivationFunctionType
+AX = mybir.AxisListType
+
+P = 128
+M = 8192
+K = 512
+BLK = 64
+EPS = 1e-6
+T_PER_P = M // P
+TL = 4
+CH = TL * P
+NCH = M // CH
+NJ = 4
+AHEAD = 4
+
+FLOPS = 2 * 2 * M * K * K
+
+PIN = True
+
+
+def tile_treelayer_t_kernel(tc, x, x_init, treeWeights, breezeBiasWeights, out):
+    nc = tc.nc
+    x_rows = x.rearrange("(p t) k -> p (t k)", t=T_PER_P)
+    c_rows = x_init.rearrange("(p t) n -> p (t n)", t=T_PER_P)
+    out_rows = out.rearrange("(p t) n -> p t n", t=T_PER_P)
+
+    with ExitStack() as ctx:
+        if PIN:
+            ctx.enter_context(tc.manual_schedule())
+        keep = ctx.enter_context(tc.tile_pool(name="keep", bufs=1))
+
+        ident = keep.tile([P, P], F32, name="ident")
+        wc = keep.tile([P, K], U32, name="wc", align_bytes=64)
+        ws = keep.tile([P, K], U8, name="ws", align_bytes=64)
+        sums = keep.tile([P, NJ, NCH], F32, name="sums")
+        sqs = keep.tile([P, NJ, NCH], F32, name="sqs")
+        negs = keep.tile([P, NJ], F32, name="negs")
+        warm = keep.tile([P, 1], F32, name="warm")
+        warm2 = keep.tile([P, 1], F32, name="warm2")
+        h = []
+        for c in range(NCH):
+            hc = keep.tile([P, NJ, CH], F32, name="h%d" % c)
+            h.append(hc)
+
+        with ExitStack() as ph1:
+            stage = ph1.enter_context(tc.tile_pool(name="stage", bufs=1))
+            psum = ph1.enter_context(tc.psum_pool(name="psum", bufs=1))
+
+            tw = stage.tile([P, 4, K], BF16, name="tw")
+            bw = stage.tile([P, 4, K], BF16, name="bw")
+            wg = stage.tile([P, 4 * K], BF16, name="wg", align_bytes=64)
+            junk = stage.tile([P, CH], F32, name="junk")
+
+            xs = {}
+            cs = {}
+            xts = {}
+            cts = {}
+            grp = {}
+            cT = {}
+            xc = {}
+            xsc = {}
+            gb = {}
+            pending = []
+            squared = [0]
+
+            def load(c):
+                xs_t = stage.tile([P, TL * K], BF16, name="xs", tag="xs", bufs=AHEAD)
+                nc.sync.dma_start(out=xs_t[:], in_=x_rows[:, c * TL * K : (c + 1) * TL * K])
+                xs[c] = xs_t
+                cs_t = stage.tile([P, TL * K], BF16, name="cs", tag="cs", bufs=AHEAD)
+                nc.sync.dma_start(out=cs_t[:], in_=c_rows[:, c * TL * K : (c + 1) * TL * K])
+                cs[c] = cs_t
+
+            def transposes(c):
+                x32 = xs[c][:].bitcast(F32)
+                for b in range(2):
+                    xt = psum.tile([P, CH], F32, name="xt", tag="xt", bufs=2)
+                    for r in range(2):
+                        for u in range(2):
+                            src = (2 * b + r) * 256 + u * P
+                            dst = u * 256 + r * P
+                            nc.tensor.transpose(xt[:, dst : dst + P], x32[:, src : src + P], ident[:])
+                    xts[c, b] = xt
+                c32 = cs[c][:].bitcast(F32)
+                for u in range(2):
+                    ct = psum.tile([P, CH], F32, name="ct", tag="ct", bufs=2)
+                    for tl in range(TL):
+                        src = tl * 256 + u * P
+                        nc.tensor.transpose(ct[:, tl * P : (tl + 1) * P], c32[:, src : src + P], ident[:])
+                    cts[c, u] = ct
+                grp_t = stage.tile([P, 4 * CH], BF16, name="grp", tag="grp", bufs=3, align_bytes=64)
+                grp[c] = grp_t
+                cT_t = stage.tile([P, 2 * CH], F32, name="cT", tag="cT", bufs=3)
+                cT[c] = cT_t
+
+            def copy_out(on_vector, dst, src):
+                if on_vector:
+                    nc.vector.tensor_copy(out=dst, in_=src)
+                else:
+                    nc.scalar.copy(out=dst, in_=src)
+
+            def evac_x(c, b, on_vector):
+                dst = grp[c][:].bitcast(F32)[:, b * CH : (b + 1) * CH].rearrange("p (m u) -> p m u", u=2)
+                src = xts[c, b][:].rearrange("p (u m) -> p m u", u=2)
+                copy_out(on_vector, dst, src)
+
+            def evac_c(c, u, on_vector):
+                copy_out(on_vector, cT[c][:, u * CH : (u + 1) * CH], cts[c, u][:])
+
+            def quantise(c):
+                xc_t = stage.tile([P, CH], U32, name="xc", tag="xc", bufs=3, align_bytes=64)
+                xsc_t = stage.tile([P, CH], U8, name="xsc", tag="xsc", bufs=3, align_bytes=64)
+                nc.vector.quantize_mx(out=xc_t[:].bitcast(FP8X4), scales=xsc_t[:], in_=grp[c][:])
+                xc[c] = xc_t
+                xsc[c] = xsc_t
+
+            def mx(c, j):
+                g = psum.tile([P, CH], F32, name="g", tag="g", bufs=4)
+                nc.tensor.matmul_mx(
+                    out=g[:],
+                    lhsT=wc[:, j * P : (j + 1) * P].bitcast(FP8X4),
+                    lhsT_scale=ws[:, j * P : (j + 1) * P],
+                    rhs=xc[c][:].bitcast(FP8X4),
+                    rhs_scale=xsc[c][:],
+                    start=True,
+                    stop=True,
+                )
+                gb[c, j] = g
+
+            def add_init(c, j):
+                u, e = divmod(j, 2)
+                cview = cT[c][:].bitcast(BF16).rearrange("p (u m e) -> p u m e", u=2, e=2)[:, u, :, e]
+                nc.vector.scalar_tensor_tensor(
+                    out=h[c][:, j, :],
+                    in0=gb[c, j][:],
+                    scalar=(0.0 if c == 0 else negs[:, j : j + 1]),
+                    in1=cview,
+                    op0=ALU.add,
+                    op1=ALU.add,
+                    accum_out=sums[:, j, c : c + 1],
+                )
+                if c > 0:
+                    pending.append((c, j))
+
+            def pivot():
+                nc.vector.tensor_scalar(
+                    out=negs[:], in0=sums[:, :, 0], scalar1=-1.0 / CH, scalar2=None, op0=ALU.mult
+                )
+                for j in range(NJ):
+                    nc.vector.tensor_scalar(
+                        out=h[0][:, j, :], in0=h[0][:, j, :], scalar1=negs[:, j : j + 1], scalar2=None, op0=ALU.add
+                    )
+                    pending.append((0, j))
+                nc.vector.scalar_tensor_tensor(
+                    out=sums[:, :, 0], in0=negs[:], scalar=float(CH), in1=sums[:, :, 0], op0=ALU.mult, op1=ALU.add
+                )
+
+            def squares():
+                for c, j in pending[squared[0] :]:
+                    nc.scalar.activation(
+                        out=junk[:], in_=h[c][:, j, :], func=ACT.Square, accum_out=sqs[:, j, c : c + 1]
+                    )
+                squared[0] = len(pending)
+
+            nc.sync.dma_start(
+                out=bw[:].rearrange("p (u e) n -> p u e n", u=2),
+                in_=breezeBiasWeights.rearrange("(u p e) n -> p u e n", u=2, e=2),
+            )
+            nc.scalar.dma_start(
+                out=tw[:].rearrange("p (u e) n -> p u e n", u=2),
+                in_=treeWeights.rearrange("(u p e) n -> p u e n", u=2, e=2),
+            )
+            for c in range(AHEAD):
+                load(c)
+
+            make_identity(nc, ident[:])
+            nc.vector.memset(warm[:], 1.0)
+            nc.scalar.activation(out=warm2[:], in_=warm[:], func=ACT.Sqrt)
+
+            for u in range(2):
+                for q in range(4):
+                    rb = 4 * u + q
+                    rows = slice(32 * q, 32 * q + 32)
+                    if rb > 0:
+                        nc.gpsimd.memset(bw[rows, 2 * u : 2 * u + 2, 0 : BLK * rb], 0.0)
+                    blk = slice(BLK * rb, BLK * rb + BLK)
+                    nc.vector.tensor_tensor(
+                        out=bw[rows, 2 * u : 2 * u + 2, blk],
+                        in0=tw[rows, 2 * u : 2 * u + 2, blk],
+                        in1=tw[rows, 2 * u : 2 * u + 2, blk],
+                        op=ALU.mult,
+                    )
+            w_src = bw[:].rearrange("p t (u i e) -> p u e i t", u=2, e=2)
+            for j in range(NJ):
+                u, e = divmod(j, 2)
+                nc.vector.tensor_copy(
+                    out=wg[:, j * K : (j + 1) * K].rearrange("p (i t) -> p i t", t=4), in_=w_src[:, u, e]
+                )
+            nc.vector.quantize_mx(out=wc[:].bitcast(FP8X4), scales=ws[:], in_=wg[:])
+
+            for i in range(-2, NCH):
+                n2 = i + 2
+                if n2 < NCH:
+                    transposes(n2)
+                    if n2 + AHEAD < NCH:
+                        load(n2 + AHEAD)
+                    evac_x(n2, 0, False)
+                    evac_c(n2, 0, False)
+                    if n2 % 2 == 1:
+                        evac_c(n2, 1, False)
+                if i >= 0:
+                    add_init(i, 0)
+                    add_init(i, 1)
+                if -1 <= i < NCH - 1:
+                    quantise(i + 1)
+                    mx(i + 1, 0)
+                    mx(i + 1, 1)
+                squares()
+                if i >= 0:
+                    add_init(i, 2)
+                    add_init(i, 3)
+                    if i == 0:
+                        pivot()
+                if -1 <= i < NCH - 1:
+                    mx(i + 1, 2)
+                    mx(i + 1, 3)
+                if n2 < NCH:
+                    evac_x(n2, 1, True)
+                    if n2 % 2 == 0:
+                        evac_c(n2, 1, True)
+                else:
+                    squares()
+
+        s1 = keep.tile([P, NJ], F32, name="s1")
+        s2 = keep.tile([P, NJ], F32, name="s2")
+        dm = keep.tile([P, NJ], F32, name="dm")
+        d2 = keep.tile([P, NJ], F32, name="d2")
+        var = keep.tile([P, NJ], F32, name="var")
+        std = keep.tile([P, NJ], F32, name="std")
+        inv = keep.tile([P, NJ], F32, name="inv")
+        nb = keep.tile([P, NJ], F32, name="nb")
+
+        nc.vector.tensor_reduce(out=s1[:], in_=sums[:], axis=AX.X, op=ALU.add)
+        nc.vector.tensor_scalar(out=dm[:], in0=s1[:], scalar1=1.0 / M, scalar2=None, op0=ALU.mult)
+        nc.vector.tensor_tensor(out=d2[:], in0=dm[:], in1=dm[:], op=ALU.mult)
+        nc.vector.tensor_reduce(out=s2[:], in_=sqs[:], axis=AX.X, op=ALU.add)
+        nc.vector.scalar_tensor_tensor(
+            out=var[:], in0=s2[:], scalar=1.0 / M, in1=d2[:], op0=ALU.mult, op1=ALU.subtract
+        )
+        nc.vector.tensor_scalar_max(out=var[:], in0=var[:], scalar1=1e-30)
+        nc.scalar.activation(out=std[:], in_=var[:], func=ACT.Sqrt)
+        nc.scalar.activation(out=warm2[:], in_=warm[:], func=ACT.Sigmoid)
+        nc.vector.tensor_scalar_add(out=std[:], in0=std[:], scalar1=EPS)
+        nc.vector.reciprocal(out=inv[:], in_=std[:])
+        nc.vector.scalar_tensor_tensor(
+            out=nb[:], in0=dm[:], scalar=-1.0, in1=inv[:], op0=ALU.mult, op1=ALU.mult
+        )
+
+        with ExitStack() as ph2:
+            outp = ph2.enter_context(tc.tile_pool(name="outp", bufs=1))
+            psum2 = ph2.enter_context(tc.psum_pool(name="psum2", bufs=1))
+
+            def normalise(c, j, lo, hi):
+                nc.vector.tensor_scalar(
+                    out=h[c][:, j, lo:hi],
+                    in0=h[c][:, j, lo:hi],
+                    scalar1=inv[:, j : j + 1],
+                    scalar2=nb[:, j : j + 1],
+                    op0=ALU.mult,
+                    op1=ALU.add,
+                )
+
+            for c in range(NCH):
+                cuts = [0, P, CH] if c == 0 else [0, CH]
+                for lo, hi in zip(cuts[:-1], cuts[1:]):
+                    for j in range(NJ):
+                        normalise(c, j, lo, hi)
+                ost = outp.tile([P, TL, K], F32, name="ost", tag="ost", bufs=4)
+                for tl in range(TL):
+                    tr = psum2.tile([P, K], F32, name="tr", tag="tr", bufs=8)
+                    for j in range(NJ):
+                        nc.tensor.transpose(
+                            tr[:, j * P : (j + 1) * P], h[c][:, j, tl * P : (tl + 1) * P], ident[:]
+                        )
+                    nc.scalar.activation(
+                        out=ost[:, tl, :].rearrange("p (u i e) -> p u i e", u=2, e=2),
+                        in_=tr[:].rearrange("p (u e i) -> p u i e", u=2, e=2),
+                        func=ACT.Sigmoid,
+                    )
+                    if c == NCH - 1 and tl >= 1:
+                        lo = 0 if tl == 1 else tl
+                        nc.sync.dma_start(
+                            out=out_rows[:, c * TL + lo : c * TL + tl + 1, :], in_=ost[:, lo : tl + 1, :]
+                        )
+                if c < NCH - 1:
+                    nc.sync.dma_start(out=out_rows[:, c * TL : (c + 1) * TL, :], in_=ost[:])

@@ -7,6 +7,7 @@ F32 = mybir.dt.float32
 BF16 = mybir.dt.bfloat16
 U32 = mybir.dt.uint32
 U8 = mybir.dt.uint8
+I32 = mybir.dt.int32
 FP8X4 = mybir.dt.float8_e4m3fn_x4
 ALU = mybir.AluOpType
 ACT = mybir.ActivationFunctionType
@@ -27,6 +28,9 @@ AHEAD = 4
 FLOPS = 2 * 2 * M * K * K
 
 PIN = True
+N_WARM = 12
+HEAD_WARM = 3
+REPEAT = 1
 
 
 def tile_treelayer_t_kernel(tc, x, x_init, treeWeights, breezeBiasWeights, out):
@@ -48,6 +52,15 @@ def tile_treelayer_t_kernel(tc, x, x_init, treeWeights, breezeBiasWeights, out):
         negs = keep.tile([P, NJ], F32, name="negs")
         warm = keep.tile([P, 1], F32, name="warm")
         warm2 = keep.tile([P, 1], F32, name="warm2")
+        s1 = keep.tile([P, NJ], F32, name="s1")
+        s2 = keep.tile([P, NJ], F32, name="s2")
+        dm = keep.tile([P, NJ], F32, name="dm")
+        d2 = keep.tile([P, NJ], F32, name="d2")
+        var = keep.tile([P, NJ], F32, name="var")
+        std = keep.tile([P, NJ], F32, name="std")
+        inv = keep.tile([P, NJ], F32, name="inv")
+        nb = keep.tile([P, NJ], F32, name="nb")
+        nb0 = keep.tile([P, NJ], F32, name="nb0")
         h = []
         for c in range(NCH):
             hc = keep.tile([P, NJ, CH], F32, name="h%d" % c)
@@ -57,9 +70,11 @@ def tile_treelayer_t_kernel(tc, x, x_init, treeWeights, breezeBiasWeights, out):
             stage = ph1.enter_context(tc.tile_pool(name="stage", bufs=1))
             psum = ph1.enter_context(tc.psum_pool(name="psum", bufs=1))
 
-            tw = stage.tile([P, 4, K], BF16, name="tw")
-            bw = stage.tile([P, 4, K], BF16, name="bw")
+            tw = stage.tile([P, 2, 2, 256], BF16, name="tw")
+            wn = stage.tile([P, 4 * K], BF16, name="wn")
             wg = stage.tile([P, 4 * K], BF16, name="wg", align_bytes=64)
+            zc = stage.tile([P, CH], U32, name="zc", align_bytes=64)
+            zs = stage.tile([P, CH], U8, name="zs", align_bytes=64)
             junk = stage.tile([P, CH], F32, name="junk")
 
             xs = {}
@@ -82,7 +97,7 @@ def tile_treelayer_t_kernel(tc, x, x_init, treeWeights, breezeBiasWeights, out):
                 nc.sync.dma_start(out=cs_t[:], in_=c_rows[:, c * TL * K : (c + 1) * TL * K])
                 cs[c] = cs_t
 
-            def transposes(c):
+            def transposes_x(c):
                 x32 = xs[c][:].bitcast(F32)
                 for b in range(2):
                     xt = psum.tile([P, CH], F32, name="xt", tag="xt", bufs=2)
@@ -92,6 +107,10 @@ def tile_treelayer_t_kernel(tc, x, x_init, treeWeights, breezeBiasWeights, out):
                             dst = u * 256 + r * P
                             nc.tensor.transpose(xt[:, dst : dst + P], x32[:, src : src + P], ident[:])
                     xts[c, b] = xt
+                grp_t = stage.tile([P, 4 * CH], BF16, name="grp", tag="grp", bufs=3, align_bytes=64)
+                grp[c] = grp_t
+
+            def transposes_c(c):
                 c32 = cs[c][:].bitcast(F32)
                 for u in range(2):
                     ct = psum.tile([P, CH], F32, name="ct", tag="ct", bufs=2)
@@ -99,8 +118,6 @@ def tile_treelayer_t_kernel(tc, x, x_init, treeWeights, breezeBiasWeights, out):
                         src = tl * 256 + u * P
                         nc.tensor.transpose(ct[:, tl * P : (tl + 1) * P], c32[:, src : src + P], ident[:])
                     cts[c, u] = ct
-                grp_t = stage.tile([P, 4 * CH], BF16, name="grp", tag="grp", bufs=3, align_bytes=64)
-                grp[c] = grp_t
                 cT_t = stage.tile([P, 2 * CH], F32, name="cT", tag="cT", bufs=3)
                 cT[c] = cT_t
 
@@ -125,18 +142,32 @@ def tile_treelayer_t_kernel(tc, x, x_init, treeWeights, breezeBiasWeights, out):
                 xc[c] = xc_t
                 xsc[c] = xsc_t
 
-            def mx(c, j):
+            def mx(c, j, times):
                 g = psum.tile([P, CH], F32, name="g", tag="g", bufs=4)
-                nc.tensor.matmul_mx(
-                    out=g[:],
-                    lhsT=wc[:, j * P : (j + 1) * P].bitcast(FP8X4),
-                    lhsT_scale=ws[:, j * P : (j + 1) * P],
-                    rhs=xc[c][:].bitcast(FP8X4),
-                    rhs_scale=xsc[c][:],
-                    start=True,
-                    stop=True,
-                )
+                for rep in range(times):
+                    nc.tensor.matmul_mx(
+                        out=g[:],
+                        lhsT=wc[:, j * P : (j + 1) * P].bitcast(FP8X4),
+                        lhsT_scale=ws[:, j * P : (j + 1) * P],
+                        rhs=xc[c][:].bitcast(FP8X4),
+                        rhs_scale=xsc[c][:],
+                        start=True,
+                        stop=True,
+                    )
                 gb[c, j] = g
+
+            def keep_warm(n):
+                scratch = psum.tile([P, CH], F32, name="scratch", tag="g", bufs=4)
+                for rep in range(n):
+                    nc.tensor.matmul_mx(
+                        out=scratch[:],
+                        lhsT=zc[:, 0:P].bitcast(FP8X4),
+                        lhsT_scale=zs[:, 0:P],
+                        rhs=zc[:].bitcast(FP8X4),
+                        rhs_scale=zs[:],
+                        start=True,
+                        stop=True,
+                    )
 
             def add_init(c, j):
                 u, e = divmod(j, 2)
@@ -157,51 +188,57 @@ def tile_treelayer_t_kernel(tc, x, x_init, treeWeights, breezeBiasWeights, out):
                 nc.vector.tensor_scalar(
                     out=negs[:], in0=sums[:, :, 0], scalar1=-1.0 / CH, scalar2=None, op0=ALU.mult
                 )
-                for j in range(NJ):
-                    nc.vector.tensor_scalar(
-                        out=h[0][:, j, :], in0=h[0][:, j, :], scalar1=negs[:, j : j + 1], scalar2=None, op0=ALU.add
-                    )
-                    pending.append((0, j))
                 nc.vector.scalar_tensor_tensor(
                     out=sums[:, :, 0], in0=negs[:], scalar=float(CH), in1=sums[:, :, 0], op0=ALU.mult, op1=ALU.add
                 )
+                for j in range(NJ):
+                    pending.append((0, j))
 
             def squares():
                 for c, j in pending[squared[0] :]:
                     nc.scalar.activation(
-                        out=junk[:], in_=h[c][:, j, :], func=ACT.Square, accum_out=sqs[:, j, c : c + 1]
+                        out=junk[:],
+                        in_=h[c][:, j, :],
+                        func=ACT.Square,
+                        bias=(negs[:, j : j + 1] if c == 0 else 0.0),
+                        accum_out=sqs[:, j, c : c + 1],
                     )
                 squared[0] = len(pending)
 
-            nc.sync.dma_start(
-                out=bw[:].rearrange("p (u e) n -> p u e n", u=2),
-                in_=breezeBiasWeights.rearrange("(u p e) n -> p u e n", u=2, e=2),
-            )
-            nc.scalar.dma_start(
-                out=tw[:].rearrange("p (u e) n -> p u e n", u=2),
-                in_=treeWeights.rearrange("(u p e) n -> p u e n", u=2, e=2),
-            )
+            nc.vector.memset(wg[:].bitcast(I32), 0)
+            nc.vector.quantize_mx(out=zc[:].bitcast(FP8X4), scales=zs[:], in_=wg[:])
+            wn3 = wn[:].rearrange("p (t n) -> p t n", t=4)
+            for u in range(2):
+                nc.vector.memset(wn3[:, 2 * u : 2 * u + 2, 0 : 256 * u + BLK], 0.0)
+            nc.vector.memset(warm[:], 1.0)
+
+            b_src = breezeBiasWeights.rearrange("(u p e) n -> p u e n", u=2, e=2)
+            t_src = treeWeights.rearrange("(u p e) n -> p u e n", u=2, e=2)
+            for u in range(2):
+                c0 = 256 * u + BLK
+                nc.sync.dma_start(out=wn3[:, 2 * u : 2 * u + 2, c0:K], in_=b_src[:, u, :, c0:K])
+                nc.scalar.dma_start(out=tw[:, u, :, :], in_=t_src[:, u, :, 256 * u : 256 * u + 256])
             for c in range(AHEAD):
                 load(c)
 
             make_identity(nc, ident[:])
-            nc.vector.memset(warm[:], 1.0)
             nc.scalar.activation(out=warm2[:], in_=warm[:], func=ACT.Sqrt)
+            keep_warm(N_WARM)
 
             for u in range(2):
+                for q in range(2, 4):
+                    c0 = 256 * u + BLK
+                    nc.vector.memset(wn3[32 * q : 32 * q + 32, 2 * u : 2 * u + 2, c0 : c0 + BLK * (q - 1)], 0.0)
+            for u in range(2):
                 for q in range(4):
-                    rb = 4 * u + q
                     rows = slice(32 * q, 32 * q + 32)
-                    if rb > 0:
-                        nc.gpsimd.memset(bw[rows, 2 * u : 2 * u + 2, 0 : BLK * rb], 0.0)
-                    blk = slice(BLK * rb, BLK * rb + BLK)
                     nc.vector.tensor_tensor(
-                        out=bw[rows, 2 * u : 2 * u + 2, blk],
-                        in0=tw[rows, 2 * u : 2 * u + 2, blk],
-                        in1=tw[rows, 2 * u : 2 * u + 2, blk],
+                        out=wn3[rows, 2 * u : 2 * u + 2, 256 * u + BLK * q : 256 * u + BLK * q + BLK],
+                        in0=tw[rows, u, :, BLK * q : BLK * q + BLK],
+                        in1=tw[rows, u, :, BLK * q : BLK * q + BLK],
                         op=ALU.mult,
                     )
-            w_src = bw[:].rearrange("p t (u i e) -> p u e i t", u=2, e=2)
+            w_src = wn[:].rearrange("p (t u i e) -> p u e i t", t=4, u=2, e=2)
             for j in range(NJ):
                 u, e = divmod(j, 2)
                 nc.vector.tensor_copy(
@@ -209,47 +246,67 @@ def tile_treelayer_t_kernel(tc, x, x_init, treeWeights, breezeBiasWeights, out):
                 )
             nc.vector.quantize_mx(out=wc[:].bitcast(FP8X4), scales=ws[:], in_=wg[:])
 
-            for i in range(-2, NCH):
+            transposes_x(0)
+            evac_x(0, 0, False)
+            evac_x(0, 1, False)
+            keep_warm(HEAD_WARM)
+            transposes_c(0)
+            evac_c(0, 0, False)
+            evac_c(0, 1, False)
+            keep_warm(HEAD_WARM)
+            quantise(0)
+            for j in range(NJ):
+                mx(0, j, 1)
+            transposes_x(1)
+            evac_x(1, 0, False)
+            evac_x(1, 1, False)
+            transposes_c(1)
+            evac_c(1, 0, False)
+            evac_c(1, 1, False)
+            for j in range(NJ):
+                add_init(0, j)
+            pivot()
+            quantise(1)
+            transposes_x(2)
+            transposes_c(2)
+            for c in range(AHEAD, AHEAD + 3):
+                load(c)
+            evac_x(2, 0, False)
+            evac_c(2, 0, False)
+            for j in range(NJ):
+                mx(1, j, 1)
+            evac_x(2, 1, True)
+            evac_c(2, 1, True)
+            quantise(2)
+            squares()
+
+            for i in range(1, NCH):
                 n2 = i + 2
                 if n2 < NCH:
-                    transposes(n2)
+                    transposes_x(n2)
+                add_init(i, 0)
+                add_init(i, 1)
+                if i + 1 < NCH:
+                    mx(i + 1, 0, 1)
+                    mx(i + 1, 1, 1 + REPEAT)
+                if n2 < NCH:
+                    evac_x(n2, 0, False)
+                    evac_x(n2, 1, True)
+                    transposes_c(n2)
                     if n2 + AHEAD < NCH:
                         load(n2 + AHEAD)
-                    evac_x(n2, 0, False)
-                    evac_c(n2, 0, False)
-                    if n2 % 2 == 1:
-                        evac_c(n2, 1, False)
-                if i >= 0:
-                    add_init(i, 0)
-                    add_init(i, 1)
-                if -1 <= i < NCH - 1:
-                    quantise(i + 1)
-                    mx(i + 1, 0)
-                    mx(i + 1, 1)
                 squares()
-                if i >= 0:
-                    add_init(i, 2)
-                    add_init(i, 3)
-                    if i == 0:
-                        pivot()
-                if -1 <= i < NCH - 1:
-                    mx(i + 1, 2)
-                    mx(i + 1, 3)
+                add_init(i, 2)
+                add_init(i, 3)
+                if i + 1 < NCH:
+                    mx(i + 1, 2, 1)
+                    mx(i + 1, 3, 1 + REPEAT)
                 if n2 < NCH:
-                    evac_x(n2, 1, True)
-                    if n2 % 2 == 0:
-                        evac_c(n2, 1, True)
+                    evac_c(n2, 0, False)
+                    evac_c(n2, 1, n2 % 2 == 0)
+                    quantise(n2)
                 else:
                     squares()
-
-        s1 = keep.tile([P, NJ], F32, name="s1")
-        s2 = keep.tile([P, NJ], F32, name="s2")
-        dm = keep.tile([P, NJ], F32, name="dm")
-        d2 = keep.tile([P, NJ], F32, name="d2")
-        var = keep.tile([P, NJ], F32, name="var")
-        std = keep.tile([P, NJ], F32, name="std")
-        inv = keep.tile([P, NJ], F32, name="inv")
-        nb = keep.tile([P, NJ], F32, name="nb")
 
         nc.vector.tensor_reduce(out=s1[:], in_=sums[:], axis=AX.X, op=ALU.add)
         nc.vector.tensor_scalar(out=dm[:], in0=s1[:], scalar1=1.0 / M, scalar2=None, op0=ALU.mult)
@@ -266,6 +323,8 @@ def tile_treelayer_t_kernel(tc, x, x_init, treeWeights, breezeBiasWeights, out):
         nc.vector.scalar_tensor_tensor(
             out=nb[:], in0=dm[:], scalar=-1.0, in1=inv[:], op0=ALU.mult, op1=ALU.mult
         )
+        nc.vector.tensor_tensor(out=nb0[:], in0=negs[:], in1=inv[:], op=ALU.mult)
+        nc.vector.tensor_tensor(out=nb0[:], in0=nb0[:], in1=nb[:], op=ALU.add)
 
         with ExitStack() as ph2:
             outp = ph2.enter_context(tc.tile_pool(name="outp", bufs=1))
@@ -276,13 +335,14 @@ def tile_treelayer_t_kernel(tc, x, x_init, treeWeights, breezeBiasWeights, out):
                     out=h[c][:, j, lo:hi],
                     in0=h[c][:, j, lo:hi],
                     scalar1=inv[:, j : j + 1],
-                    scalar2=nb[:, j : j + 1],
+                    scalar2=(nb0 if c == 0 else nb)[:, j : j + 1],
                     op0=ALU.mult,
                     op1=ALU.add,
                 )
 
-            for c in range(NCH):
-                cuts = [0, P, CH] if c == 0 else [0, CH]
+            order = list(range(1, NCH)) + [0]
+            for c in order:
+                cuts = [0, P, CH] if c == order[0] else [0, CH]
                 for lo, hi in zip(cuts[:-1], cuts[1:]):
                     for j in range(NJ):
                         normalise(c, j, lo, hi)
@@ -298,10 +358,10 @@ def tile_treelayer_t_kernel(tc, x, x_init, treeWeights, breezeBiasWeights, out):
                         in_=tr[:].rearrange("p (u e i) -> p u i e", u=2, e=2),
                         func=ACT.Sigmoid,
                     )
-                    if c == NCH - 1 and tl >= 1:
+                    if c == order[-1] and tl >= 1:
                         lo = 0 if tl == 1 else tl
                         nc.sync.dma_start(
                             out=out_rows[:, c * TL + lo : c * TL + tl + 1, :], in_=ost[:, lo : tl + 1, :]
                         )
-                if c < NCH - 1:
+                if c != order[-1]:
                     nc.sync.dma_start(out=out_rows[:, c * TL : (c + 1) * TL, :], in_=ost[:])

@@ -89,10 +89,12 @@ def tile_treelayer_t_kernel(tc, x, x_init, treeWeights, breezeBiasWeights, out):
             pending = []
             squared = [0]
 
-            def load(c):
+            def load_x(c):
                 xs_t = stage.tile([P, TL * K], BF16, name="xs", tag="xs", bufs=AHEAD)
                 nc.sync.dma_start(out=xs_t[:], in_=x_rows[:, c * TL * K : (c + 1) * TL * K])
                 xs[c] = xs_t
+
+            def load_c(c):
                 cs_t = stage.tile([P, TL * K], BF16, name="cs", tag="cs", bufs=AHEAD)
                 nc.sync.dma_start(out=cs_t[:], in_=c_rows[:, c * TL * K : (c + 1) * TL * K])
                 cs[c] = cs_t
@@ -109,6 +111,8 @@ def tile_treelayer_t_kernel(tc, x, x_init, treeWeights, breezeBiasWeights, out):
                     xts[c, b] = xt
                 grp_t = stage.tile([P, 4 * CH], BF16, name="grp", tag="grp", bufs=3, align_bytes=64)
                 grp[c] = grp_t
+                if c + AHEAD < NCH:
+                    load_x(c + AHEAD)
 
             def transposes_c(c):
                 c32 = cs[c][:].bitcast(F32)
@@ -120,6 +124,8 @@ def tile_treelayer_t_kernel(tc, x, x_init, treeWeights, breezeBiasWeights, out):
                     cts[c, u] = ct
                 cT_t = stage.tile([P, 2 * CH], F32, name="cT", tag="cT", bufs=3)
                 cT[c] = cT_t
+                if c + AHEAD < NCH:
+                    load_c(c + AHEAD)
 
             def copy_out(on_vector, dst, src):
                 if on_vector:
@@ -219,7 +225,8 @@ def tile_treelayer_t_kernel(tc, x, x_init, treeWeights, breezeBiasWeights, out):
                 nc.sync.dma_start(out=wn3[:, 2 * u : 2 * u + 2, c0:K], in_=b_src[:, u, :, c0:K])
                 nc.scalar.dma_start(out=tw[:, u, :, :], in_=t_src[:, u, :, 256 * u : 256 * u + 256])
             for c in range(AHEAD):
-                load(c)
+                load_x(c)
+                load_c(c)
 
             make_identity(nc, ident[:])
             nc.scalar.activation(out=warm2[:], in_=warm[:], func=ACT.Sqrt)
@@ -269,21 +276,20 @@ def tile_treelayer_t_kernel(tc, x, x_init, treeWeights, breezeBiasWeights, out):
             quantise(1)
             transposes_x(2)
             transposes_c(2)
-            for c in range(AHEAD, AHEAD + 3):
-                load(c)
             evac_x(2, 0, False)
             evac_c(2, 0, False)
             for j in range(NJ):
                 mx(1, j, 1)
             evac_x(2, 1, True)
             evac_c(2, 1, True)
+            transposes_x(3)
             quantise(2)
             squares()
 
             for i in range(1, NCH):
                 n2 = i + 2
                 if n2 < NCH:
-                    transposes_x(n2)
+                    transposes_c(n2)
                 add_init(i, 0)
                 add_init(i, 1)
                 if i + 1 < NCH:
@@ -292,9 +298,8 @@ def tile_treelayer_t_kernel(tc, x, x_init, treeWeights, breezeBiasWeights, out):
                 if n2 < NCH:
                     evac_x(n2, 0, False)
                     evac_x(n2, 1, True)
-                    transposes_c(n2)
-                    if n2 + AHEAD < NCH:
-                        load(n2 + AHEAD)
+                if n2 + 1 < NCH:
+                    transposes_x(n2 + 1)
                 squares()
                 add_init(i, 2)
                 add_init(i, 3)

@@ -31,6 +31,9 @@ PIN = True
 N_WARM = 12
 HEAD_WARM = 3
 REPEAT = 1
+G_CHUNKS = list(range(1, 15))
+WIDE_SECOND = list(range(2, 13, 2))
+NSQ = 10
 
 
 def tile_treelayer_t_kernel(tc, x, x_init, treeWeights, breezeBiasWeights, out):
@@ -48,8 +51,9 @@ def tile_treelayer_t_kernel(tc, x, x_init, treeWeights, breezeBiasWeights, out):
         wc = keep.tile([P, K], U32, name="wc", align_bytes=64)
         ws = keep.tile([P, K], U8, name="ws", align_bytes=64)
         sums = keep.tile([P, NJ, NCH], F32, name="sums")
-        sqs = keep.tile([P, NJ, NCH], F32, name="sqs")
+        sqs = keep.tile([P, NJ, NSQ], F32, name="sqs")
         negs = keep.tile([P, NJ], F32, name="negs")
+        gsum = keep.tile([P, NJ], F32, name="gsum")
         warm = keep.tile([P, 1], F32, name="warm")
         warm2 = keep.tile([P, 1], F32, name="warm2")
         s1 = keep.tile([P, NJ], F32, name="s1")
@@ -61,10 +65,15 @@ def tile_treelayer_t_kernel(tc, x, x_init, treeWeights, breezeBiasWeights, out):
         inv = keep.tile([P, NJ], F32, name="inv")
         nb = keep.tile([P, NJ], F32, name="nb")
         nb0 = keep.tile([P, NJ], F32, name="nb0")
-        h = []
-        for c in range(NCH):
-            hc = keep.tile([P, NJ, CH], F32, name="h%d" % c)
-            h.append(hc)
+        h_tiles = []
+        for g in range(NCH // 2 + 1):
+            width = CH if g in (0, NCH // 2) else 2 * CH
+            hg = keep.tile([P, NJ, width], F32, name="h%d" % g)
+            h_tiles.append(hg)
+
+        def h_at(c, j, lo, hi):
+            off = CH if (c > 0 and c % 2 == 0) else 0
+            return h_tiles[(c + 1) // 2][:, j, off + lo : off + hi]
 
         with ExitStack() as ph1:
             stage = ph1.enter_context(tc.tile_pool(name="stage", bufs=1))
@@ -75,7 +84,9 @@ def tile_treelayer_t_kernel(tc, x, x_init, treeWeights, breezeBiasWeights, out):
             wg = stage.tile([P, 4 * K], BF16, name="wg", align_bytes=64)
             zc = stage.tile([P, CH], U32, name="zc", align_bytes=64)
             zs = stage.tile([P, CH], U8, name="zs", align_bytes=64)
-            junk = stage.tile([P, CH], F32, name="junk")
+            junk = stage.tile([P, 2 * CH], F32, name="junk")
+            gsq = stage.tile([P, CH], F32, name="gsq")
+            gacc = stage.tile([P, CH], F32, name="gacc")
 
             xs = {}
             cs = {}
@@ -88,6 +99,7 @@ def tile_treelayer_t_kernel(tc, x, x_init, treeWeights, breezeBiasWeights, out):
             gb = {}
             pending = []
             squared = [0]
+            n_sq = [0] * NJ
 
             def load_x(c):
                 xs_t = stage.tile([P, TL * K], BF16, name="xs", tag="xs", bufs=AHEAD)
@@ -179,7 +191,7 @@ def tile_treelayer_t_kernel(tc, x, x_init, treeWeights, breezeBiasWeights, out):
                 u, e = divmod(j, 2)
                 cview = cT[c][:].bitcast(BF16).rearrange("p (u m e) -> p u m e", u=2, e=2)[:, u, :, e]
                 nc.vector.scalar_tensor_tensor(
-                    out=h[c][:, j, :],
+                    out=h_at(c, j, 0, CH),
                     in0=gb[c, j][:],
                     scalar=(0.0 if c == 0 else negs[:, j : j + 1]),
                     in1=cview,
@@ -187,8 +199,17 @@ def tile_treelayer_t_kernel(tc, x, x_init, treeWeights, breezeBiasWeights, out):
                     op1=ALU.add,
                     accum_out=sums[:, j, c : c + 1],
                 )
-                if c > 0:
-                    pending.append((c, j))
+                if j == 0 and c in G_CHUNKS:
+                    first = c == G_CHUNKS[0]
+                    nc.gpsimd.tensor_tensor(
+                        out=(gacc if first else gsq)[:], in0=h_at(c, j, 0, CH), in1=h_at(c, j, 0, CH), op=ALU.mult
+                    )
+                    if not first:
+                        nc.gpsimd.tensor_tensor(out=gacc[:], in0=gacc[:], in1=gsq[:], op=ALU.add)
+                elif c in WIDE_SECOND:
+                    pending.append((c - 1, j, 2 * CH))
+                elif c > 0 and c + 1 not in WIDE_SECOND:
+                    pending.append((c, j, CH))
 
             def pivot():
                 nc.vector.tensor_scalar(
@@ -198,17 +219,18 @@ def tile_treelayer_t_kernel(tc, x, x_init, treeWeights, breezeBiasWeights, out):
                     out=sums[:, :, 0], in0=negs[:], scalar=float(CH), in1=sums[:, :, 0], op0=ALU.mult, op1=ALU.add
                 )
                 for j in range(NJ):
-                    pending.append((0, j))
+                    pending.append((0, j, CH))
 
             def squares():
-                for c, j in pending[squared[0] :]:
+                for c, j, width in pending[squared[0] :]:
                     nc.scalar.activation(
-                        out=junk[:],
-                        in_=h[c][:, j, :],
+                        out=junk[:, 0:width],
+                        in_=h_at(c, j, 0, width),
                         func=ACT.Square,
                         bias=(negs[:, j : j + 1] if c == 0 else 0.0),
-                        accum_out=sqs[:, j, c : c + 1],
+                        accum_out=sqs[:, j, n_sq[j] : n_sq[j] + 1],
                     )
+                    n_sq[j] += 1
                 squared[0] = len(pending)
 
             nc.vector.memset(wg[:].bitcast(I32), 0)
@@ -217,6 +239,8 @@ def tile_treelayer_t_kernel(tc, x, x_init, treeWeights, breezeBiasWeights, out):
             for u in range(2):
                 nc.vector.memset(wn3[:, 2 * u : 2 * u + 2, 0 : 256 * u + BLK], 0.0)
             nc.vector.memset(warm[:], 1.0)
+            nc.vector.memset(sqs[:], 0.0)
+            nc.vector.memset(gsum[:], 0.0)
 
             b_src = breezeBiasWeights.rearrange("(u p e) n -> p u e n", u=2, e=2)
             t_src = treeWeights.rearrange("(u p e) n -> p u e n", u=2, e=2)
@@ -308,14 +332,17 @@ def tile_treelayer_t_kernel(tc, x, x_init, treeWeights, breezeBiasWeights, out):
                     mx(i + 1, 3, 1 + REPEAT)
                 if n2 < NCH:
                     evac_c(n2, 0, False)
-                    evac_c(n2, 1, n2 % 2 == 0)
+                    evac_c(n2, 1, False)
                     quantise(n2)
                 else:
                     squares()
 
+            nc.vector.tensor_reduce(out=gsum[:, 0:1], in_=gacc[:], axis=AX.X, op=ALU.add)
+
         nc.vector.tensor_reduce(out=s1[:], in_=sums[:], axis=AX.X, op=ALU.add)
         nc.vector.tensor_scalar(out=dm[:], in0=s1[:], scalar1=1.0 / M, scalar2=None, op0=ALU.mult)
         nc.vector.tensor_tensor(out=d2[:], in0=dm[:], in1=dm[:], op=ALU.mult)
+        nc.vector.scalar_tensor_tensor(out=d2[:], in0=gsum[:], scalar=-1.0 / M, in1=d2[:], op0=ALU.mult, op1=ALU.add)
         nc.vector.tensor_reduce(out=s2[:], in_=sqs[:], axis=AX.X, op=ALU.add)
         nc.vector.scalar_tensor_tensor(
             out=var[:], in0=s2[:], scalar=1.0 / M, in1=d2[:], op0=ALU.mult, op1=ALU.subtract
@@ -337,8 +364,8 @@ def tile_treelayer_t_kernel(tc, x, x_init, treeWeights, breezeBiasWeights, out):
 
             def normalise(c, j, lo, hi):
                 nc.vector.tensor_scalar(
-                    out=h[c][:, j, lo:hi],
-                    in0=h[c][:, j, lo:hi],
+                    out=h_at(c, j, lo, hi),
+                    in0=h_at(c, j, lo, hi),
                     scalar1=inv[:, j : j + 1],
                     scalar2=(nb0 if c == 0 else nb)[:, j : j + 1],
                     op0=ALU.mult,
@@ -356,7 +383,7 @@ def tile_treelayer_t_kernel(tc, x, x_init, treeWeights, breezeBiasWeights, out):
                     tr = psum2.tile([P, K], F32, name="tr", tag="tr", bufs=8)
                     for j in range(NJ):
                         nc.tensor.transpose(
-                            tr[:, j * P : (j + 1) * P], h[c][:, j, tl * P : (tl + 1) * P], ident[:]
+                            tr[:, j * P : (j + 1) * P], h_at(c, j, tl * P, (tl + 1) * P), ident[:]
                         )
                     nc.scalar.activation(
                         out=ost[:, tl, :].rearrange("p (u i e) -> p u i e", u=2, e=2),

@@ -28,9 +28,7 @@ AHEAD = 4
 FLOPS = 2 * 2 * M * K * K
 
 PIN = True
-N_WARM = 12
-HEAD_WARM = 3
-REPEAT = 1
+REPEAT = 0
 G_CHUNKS = list(range(1, 15))
 WIDE_SECOND = list(range(2, 13, 2))
 NSQ = 10
@@ -82,9 +80,6 @@ def tile_treelayer_t_kernel(tc, x, x_init, treeWeights, breezeBiasWeights, out):
             tw = stage.tile([P, 2, 2, 256], BF16, name="tw")
             wn = stage.tile([P, 4 * K], BF16, name="wn")
             wg = stage.tile([P, 4 * K], BF16, name="wg", align_bytes=64)
-            zc = stage.tile([P, CH], U32, name="zc", align_bytes=64)
-            zs = stage.tile([P, CH], U8, name="zs", align_bytes=64)
-            junk = stage.tile([P, 2 * CH], F32, name="junk")
             gsq = stage.tile([P, CH], F32, name="gsq")
             gacc = stage.tile([P, CH], F32, name="gacc")
 
@@ -174,19 +169,6 @@ def tile_treelayer_t_kernel(tc, x, x_init, treeWeights, breezeBiasWeights, out):
                     )
                 gb[c, j] = g
 
-            def keep_warm(n):
-                scratch = psum.tile([P, CH], F32, name="scratch", tag="g", bufs=4)
-                for rep in range(n):
-                    nc.tensor.matmul_mx(
-                        out=scratch[:],
-                        lhsT=zc[:, 0:P].bitcast(FP8X4),
-                        lhsT_scale=zs[:, 0:P],
-                        rhs=zc[:].bitcast(FP8X4),
-                        rhs_scale=zs[:],
-                        start=True,
-                        stop=True,
-                    )
-
             def add_init(c, j):
                 u, e = divmod(j, 2)
                 cview = cT[c][:].bitcast(BF16).rearrange("p (u m e) -> p u m e", u=2, e=2)[:, u, :, e]
@@ -223,6 +205,7 @@ def tile_treelayer_t_kernel(tc, x, x_init, treeWeights, breezeBiasWeights, out):
 
             def squares():
                 for c, j, width in pending[squared[0] :]:
+                    junk = stage.tile([P, 2 * CH], F32, name="junk", tag="junk", bufs=4)
                     nc.scalar.activation(
                         out=junk[:, 0:width],
                         in_=h_at(c, j, 0, width),
@@ -233,8 +216,6 @@ def tile_treelayer_t_kernel(tc, x, x_init, treeWeights, breezeBiasWeights, out):
                     n_sq[j] += 1
                 squared[0] = len(pending)
 
-            nc.vector.memset(wg[:].bitcast(I32), 0)
-            nc.vector.quantize_mx(out=zc[:].bitcast(FP8X4), scales=zs[:], in_=wg[:])
             wn3 = wn[:].rearrange("p (t n) -> p t n", t=4)
             for u in range(2):
                 nc.vector.memset(wn3[:, 2 * u : 2 * u + 2, 0 : 256 * u + BLK], 0.0)
@@ -254,7 +235,6 @@ def tile_treelayer_t_kernel(tc, x, x_init, treeWeights, breezeBiasWeights, out):
 
             make_identity(nc, ident[:])
             nc.scalar.activation(out=warm2[:], in_=warm[:], func=ACT.Sqrt)
-            keep_warm(N_WARM)
 
             for u in range(2):
                 for q in range(2, 4):
@@ -280,11 +260,9 @@ def tile_treelayer_t_kernel(tc, x, x_init, treeWeights, breezeBiasWeights, out):
             transposes_x(0)
             evac_x(0, 0, False)
             evac_x(0, 1, False)
-            keep_warm(HEAD_WARM)
             transposes_c(0)
             evac_c(0, 0, False)
             evac_c(0, 1, False)
-            keep_warm(HEAD_WARM)
             quantise(0)
             for j in range(NJ):
                 mx(0, j, 1)

@@ -351,11 +351,12 @@ def tile_treelayer_t_kernel(tc, x, x_init, treeWeights, breezeBiasWeights, out):
                 )
 
             order = list(range(1, NCH)) + [0]
-            for c in order:
+            for k, c in enumerate(order + order):
                 cuts = [0, P, CH] if c == order[0] else [0, CH]
                 for lo, hi in zip(cuts[:-1], cuts[1:]):
                     for j in range(NJ):
-                        normalise(c, j, lo, hi)
+                        if k < NCH:
+                            normalise(c, j, lo, hi)
                 ost = outp.tile([P, TL, K], F32, name="ost", tag="ost", bufs=4)
                 for tl in range(TL):
                     tr = psum2.tile([P, K], F32, name="tr", tag="tr", bufs=8)

@@ -7,7 +7,6 @@ F32 = mybir.dt.float32
 BF16 = mybir.dt.bfloat16
 U32 = mybir.dt.uint32
 U8 = mybir.dt.uint8
-I32 = mybir.dt.int32
 FP8X4 = mybir.dt.float8_e4m3fn_x4
 ALU = mybir.AluOpType
 ACT = mybir.ActivationFunctionType
@@ -17,122 +16,126 @@ P = 128
 M = 8192
 K = 512
 BLK = 64
+HALF = K // 2
 EPS = 1e-6
-T_PER_P = M // P
+TINY = 1e-30
+ROWS_PER_PARTITION = M // P
 TL = 4
 CH = TL * P
 NCH = M // CH
-NJ = 4
+NJ = K // P
 AHEAD = 4
 
 FLOPS = 2 * 2 * M * K * K
 
-PIN = True
-REPEAT = 0
-G_CHUNKS = list(range(1, 15))
-WIDE_SECOND = list(range(2, 13, 2))
-NSQ = 10
+GPSIMD_PIECES = [(c, 0) for c in range(1, NCH)] + [(1, 1), (3, 1)]
+VECTOR_PIECES = [(NCH - 1, 2)]
+PAIR_FIRST = list(range(1, 12, 2))
+SQ_COLS = 10
+VECTOR_EVERY = 4
 
 
 def tile_treelayer_t_kernel(tc, x, x_init, treeWeights, breezeBiasWeights, out):
     nc = tc.nc
-    x_rows = x.rearrange("(p t) k -> p (t k)", t=T_PER_P)
-    c_rows = x_init.rearrange("(p t) n -> p (t n)", t=T_PER_P)
-    out_rows = out.rearrange("(p t) n -> p t n", t=T_PER_P)
+    x_rows = x.rearrange("(p t) k -> p (t k)", t=ROWS_PER_PARTITION)
+    init_rows = x_init.rearrange("(p t) n -> p (t n)", t=ROWS_PER_PARTITION)
+    out_rows = out.rearrange("(p t) n -> p t n", t=ROWS_PER_PARTITION)
 
     with ExitStack() as ctx:
-        if PIN:
-            ctx.enter_context(tc.manual_schedule())
+        ctx.enter_context(tc.manual_schedule())
         keep = ctx.enter_context(tc.tile_pool(name="keep", bufs=1))
 
         ident = keep.tile([P, P], F32, name="ident")
-        wc = keep.tile([P, K], U32, name="wc", align_bytes=64)
-        ws = keep.tile([P, K], U8, name="ws", align_bytes=64)
-        sums = keep.tile([P, NJ, NCH], F32, name="sums")
-        sqs = keep.tile([P, NJ, NSQ], F32, name="sqs")
-        negs = keep.tile([P, NJ], F32, name="negs")
-        gsum = keep.tile([P, NJ], F32, name="gsum")
-        warm = keep.tile([P, 1], F32, name="warm")
-        warm2 = keep.tile([P, 1], F32, name="warm2")
-        s1 = keep.tile([P, NJ], F32, name="s1")
-        s2 = keep.tile([P, NJ], F32, name="s2")
-        dm = keep.tile([P, NJ], F32, name="dm")
-        d2 = keep.tile([P, NJ], F32, name="d2")
+        w_words = keep.tile([P, K], U32, name="w_words", align_bytes=64)
+        w_scales = keep.tile([P, K], U8, name="w_scales", align_bytes=64)
+        sum_h = keep.tile([P, NJ, NCH], F32, name="sum_h")
+        sum_sq = keep.tile([P, NJ, SQ_COLS], F32, name="sum_sq")
+        sum_sq_g = keep.tile([P, NJ], F32, name="sum_sq_g")
+        sum_sq_v = keep.tile([P, NJ], F32, name="sum_sq_v")
+        neg_pivot = keep.tile([P, NJ], F32, name="neg_pivot")
+        one = keep.tile([P, 1], F32, name="one")
+        unused = keep.tile([P, 1], F32, name="unused")
+        total_h = keep.tile([P, NJ], F32, name="total_h")
+        total_sq = keep.tile([P, NJ], F32, name="total_sq")
+        mean = keep.tile([P, NJ], F32, name="mean")
+        less = keep.tile([P, NJ], F32, name="less")
         var = keep.tile([P, NJ], F32, name="var")
         std = keep.tile([P, NJ], F32, name="std")
-        inv = keep.tile([P, NJ], F32, name="inv")
-        nb = keep.tile([P, NJ], F32, name="nb")
-        nb0 = keep.tile([P, NJ], F32, name="nb0")
-        h_tiles = []
-        for g in range(NCH // 2 + 1):
-            width = CH if g in (0, NCH // 2) else 2 * CH
-            hg = keep.tile([P, NJ, width], F32, name="h%d" % g)
-            h_tiles.append(hg)
+        scale = keep.tile([P, NJ], F32, name="scale")
+        bias = keep.tile([P, NJ], F32, name="bias")
+        bias0 = keep.tile([P, NJ], F32, name="bias0")
+
+        h_home = {}
+        for first, count in [(0, 1)] + [(c, 2) for c in range(1, NCH - 1, 2)] + [(NCH - 1, 1)]:
+            h_tile = keep.tile([P, NJ, count * CH], F32, name="h%d" % first)
+            for c in range(first, first + count):
+                h_home[c] = (h_tile, (c - first) * CH)
 
         def h_at(c, j, lo, hi):
-            off = CH if (c > 0 and c % 2 == 0) else 0
-            return h_tiles[(c + 1) // 2][:, j, off + lo : off + hi]
+            h_tile, off = h_home[c]
+            return h_tile[:, j, off + lo : off + hi]
 
         with ExitStack() as ph1:
             stage = ph1.enter_context(tc.tile_pool(name="stage", bufs=1))
             psum = ph1.enter_context(tc.psum_pool(name="psum", bufs=1))
 
-            tw = stage.tile([P, 2, 2, 256], BF16, name="tw")
-            wn = stage.tile([P, 4 * K], BF16, name="wn")
-            wg = stage.tile([P, 4 * K], BF16, name="wg", align_bytes=64)
-            gsq = stage.tile([P, CH], F32, name="gsq")
-            gacc = stage.tile([P, CH], F32, name="gacc")
+            t_raw = stage.tile([P, 2, 2, HALF], BF16, name="t_raw")
+            w_rows = stage.tile([P, 4 * K], BF16, name="w_rows")
+            w_grouped = stage.tile([P, 4 * K], BF16, name="w_grouped", align_bytes=64)
+            g_square = stage.tile([P, CH], F32, name="g_square")
+            v_square = stage.tile([P, CH], F32, name="v_square")
 
-            xs = {}
-            cs = {}
-            xts = {}
-            cts = {}
-            grp = {}
-            cT = {}
-            xc = {}
-            xsc = {}
-            gb = {}
-            pending = []
+            x_nat = {}
+            init_nat = {}
+            x_banks = {}
+            init_banks = {}
+            x_grouped = {}
+            init_t = {}
+            x_words = {}
+            x_scales = {}
+            product = {}
+            g_running = {}
+            for_scalar = []
             squared = [0]
-            n_sq = [0] * NJ
+            sq_used = [0] * NJ
 
             def load_x(c):
-                xs_t = stage.tile([P, TL * K], BF16, name="xs", tag="xs", bufs=AHEAD)
-                nc.sync.dma_start(out=xs_t[:], in_=x_rows[:, c * TL * K : (c + 1) * TL * K])
-                xs[c] = xs_t
+                x_nat_t = stage.tile([P, TL * K], BF16, name="x_nat", tag="x_nat", bufs=AHEAD)
+                nc.sync.dma_start(out=x_nat_t[:], in_=x_rows[:, c * TL * K : (c + 1) * TL * K])
+                x_nat[c] = x_nat_t
 
-            def load_c(c):
-                cs_t = stage.tile([P, TL * K], BF16, name="cs", tag="cs", bufs=AHEAD)
-                nc.sync.dma_start(out=cs_t[:], in_=c_rows[:, c * TL * K : (c + 1) * TL * K])
-                cs[c] = cs_t
+            def load_init(c):
+                init_nat_t = stage.tile([P, TL * K], BF16, name="init_nat", tag="init_nat", bufs=AHEAD)
+                nc.sync.dma_start(out=init_nat_t[:], in_=init_rows[:, c * TL * K : (c + 1) * TL * K])
+                init_nat[c] = init_nat_t
 
-            def transposes_x(c):
-                x32 = xs[c][:].bitcast(F32)
+            def transpose_x(c):
+                words = x_nat[c][:].bitcast(F32)
                 for b in range(2):
-                    xt = psum.tile([P, CH], F32, name="xt", tag="xt", bufs=2)
+                    bank = psum.tile([P, CH], F32, name="x_bank", tag="x_bank", bufs=2)
                     for r in range(2):
                         for u in range(2):
-                            src = (2 * b + r) * 256 + u * P
-                            dst = u * 256 + r * P
-                            nc.tensor.transpose(xt[:, dst : dst + P], x32[:, src : src + P], ident[:])
-                    xts[c, b] = xt
-                grp_t = stage.tile([P, 4 * CH], BF16, name="grp", tag="grp", bufs=3, align_bytes=64)
-                grp[c] = grp_t
+                            src = (2 * b + r) * HALF + u * P
+                            dst = u * HALF + r * P
+                            nc.tensor.transpose(bank[:, dst : dst + P], words[:, src : src + P], ident[:])
+                    x_banks[c, b] = bank
+                x_grouped_t = stage.tile([P, 4 * CH], BF16, name="x_grouped", tag="x_grouped", bufs=3, align_bytes=64)
+                x_grouped[c] = x_grouped_t
                 if c + AHEAD < NCH:
                     load_x(c + AHEAD)
 
-            def transposes_c(c):
-                c32 = cs[c][:].bitcast(F32)
+            def transpose_init(c):
+                words = init_nat[c][:].bitcast(F32)
                 for u in range(2):
-                    ct = psum.tile([P, CH], F32, name="ct", tag="ct", bufs=2)
+                    bank = psum.tile([P, CH], F32, name="init_bank", tag="init_bank", bufs=2)
                     for tl in range(TL):
-                        src = tl * 256 + u * P
-                        nc.tensor.transpose(ct[:, tl * P : (tl + 1) * P], c32[:, src : src + P], ident[:])
-                    cts[c, u] = ct
-                cT_t = stage.tile([P, 2 * CH], F32, name="cT", tag="cT", bufs=3)
-                cT[c] = cT_t
+                        src = tl * HALF + u * P
+                        nc.tensor.transpose(bank[:, tl * P : (tl + 1) * P], words[:, src : src + P], ident[:])
+                    init_banks[c, u] = bank
+                init_t_t = stage.tile([P, 2 * CH], F32, name="init_t", tag="init_t", bufs=3)
+                init_t[c] = init_t_t
                 if c + AHEAD < NCH:
-                    load_c(c + AHEAD)
+                    load_init(c + AHEAD)
 
             def copy_out(on_vector, dst, src):
                 if on_vector:
@@ -140,201 +143,229 @@ def tile_treelayer_t_kernel(tc, x, x_init, treeWeights, breezeBiasWeights, out):
                 else:
                     nc.scalar.copy(out=dst, in_=src)
 
-            def evac_x(c, b, on_vector):
-                dst = grp[c][:].bitcast(F32)[:, b * CH : (b + 1) * CH].rearrange("p (m u) -> p m u", u=2)
-                src = xts[c, b][:].rearrange("p (u m) -> p m u", u=2)
+            def empty_x_bank(c, b, on_vector):
+                dst = x_grouped[c][:].bitcast(F32)[:, b * CH : (b + 1) * CH].rearrange("p (m u) -> p m u", u=2)
+                src = x_banks[c, b][:].rearrange("p (u m) -> p m u", u=2)
                 copy_out(on_vector, dst, src)
 
-            def evac_c(c, u, on_vector):
-                copy_out(on_vector, cT[c][:, u * CH : (u + 1) * CH], cts[c, u][:])
+            def empty_init_bank(c, u):
+                copy_out(False, init_t[c][:, u * CH : (u + 1) * CH], init_banks[c, u][:])
 
-            def quantise(c):
-                xc_t = stage.tile([P, CH], U32, name="xc", tag="xc", bufs=3, align_bytes=64)
-                xsc_t = stage.tile([P, CH], U8, name="xsc", tag="xsc", bufs=3, align_bytes=64)
-                nc.vector.quantize_mx(out=xc_t[:].bitcast(FP8X4), scales=xsc_t[:], in_=grp[c][:])
-                xc[c] = xc_t
-                xsc[c] = xsc_t
+            def quantise_x(c):
+                words = stage.tile([P, CH], U32, name="x_words", tag="x_words", bufs=3, align_bytes=64)
+                scales = stage.tile([P, CH], U8, name="x_scales", tag="x_scales", bufs=3, align_bytes=64)
+                nc.vector.quantize_mx(out=words[:].bitcast(FP8X4), scales=scales[:], in_=x_grouped[c][:])
+                x_words[c] = words
+                x_scales[c] = scales
 
-            def mx(c, j, times):
-                g = psum.tile([P, CH], F32, name="g", tag="g", bufs=4)
-                for rep in range(times):
-                    nc.tensor.matmul_mx(
-                        out=g[:],
-                        lhsT=wc[:, j * P : (j + 1) * P].bitcast(FP8X4),
-                        lhsT_scale=ws[:, j * P : (j + 1) * P],
-                        rhs=xc[c][:].bitcast(FP8X4),
-                        rhs_scale=xsc[c][:],
-                        start=True,
-                        stop=True,
-                    )
-                gb[c, j] = g
+            def multiply(c, j):
+                acc = psum.tile([P, CH], F32, name="acc", tag="acc", bufs=4)
+                nc.tensor.matmul_mx(
+                    out=acc[:],
+                    lhsT=w_words[:, j * P : (j + 1) * P].bitcast(FP8X4),
+                    lhsT_scale=w_scales[:, j * P : (j + 1) * P],
+                    rhs=x_words[c][:].bitcast(FP8X4),
+                    rhs_scale=x_scales[c][:],
+                    start=True,
+                    stop=True,
+                )
+                product[c, j] = acc
+
+            def on_scalar(c, j):
+                return (c, j) not in GPSIMD_PIECES and (c, j) not in VECTOR_PIECES
 
             def add_init(c, j):
                 u, e = divmod(j, 2)
-                cview = cT[c][:].bitcast(BF16).rearrange("p (u m e) -> p u m e", u=2, e=2)[:, u, :, e]
+                init_view = init_t[c][:].bitcast(BF16).rearrange("p (u m e) -> p u m e", u=2, e=2)[:, u, :, e]
                 nc.vector.scalar_tensor_tensor(
                     out=h_at(c, j, 0, CH),
-                    in0=gb[c, j][:],
-                    scalar=(0.0 if c == 0 else negs[:, j : j + 1]),
-                    in1=cview,
+                    in0=product[c, j][:],
+                    scalar=(0.0 if c == 0 else neg_pivot[:, j : j + 1]),
+                    in1=init_view,
                     op0=ALU.add,
                     op1=ALU.add,
-                    accum_out=sums[:, j, c : c + 1],
+                    accum_out=sum_h[:, j, c : c + 1],
                 )
-                if j == 0 and c in G_CHUNKS:
-                    first = c == G_CHUNKS[0]
+                if (c, j) in GPSIMD_PIECES:
+                    first = j not in g_running
+                    if first:
+                        running = stage.tile([P, CH], F32, name="g_running%d" % j)
+                        g_running[j] = running
                     nc.gpsimd.tensor_tensor(
-                        out=(gacc if first else gsq)[:], in0=h_at(c, j, 0, CH), in1=h_at(c, j, 0, CH), op=ALU.mult
+                        out=(g_running[j] if first else g_square)[:],
+                        in0=h_at(c, j, 0, CH),
+                        in1=h_at(c, j, 0, CH),
+                        op=ALU.mult,
                     )
                     if not first:
-                        nc.gpsimd.tensor_tensor(out=gacc[:], in0=gacc[:], in1=gsq[:], op=ALU.add)
-                elif c in WIDE_SECOND:
-                    pending.append((c - 1, j, 2 * CH))
-                elif c > 0 and c + 1 not in WIDE_SECOND:
-                    pending.append((c, j, CH))
+                        nc.gpsimd.tensor_tensor(out=g_running[j][:], in0=g_running[j][:], in1=g_square[:], op=ALU.add)
+                elif c > 0 and on_scalar(c, j):
+                    if c - 1 in PAIR_FIRST and on_scalar(c - 1, j):
+                        for_scalar.append((c - 1, j, 2 * CH))
+                    elif not (c in PAIR_FIRST and on_scalar(c + 1, j)):
+                        for_scalar.append((c, j, CH))
 
-            def pivot():
+            def set_pivot():
                 nc.vector.tensor_scalar(
-                    out=negs[:], in0=sums[:, :, 0], scalar1=-1.0 / CH, scalar2=None, op0=ALU.mult
+                    out=neg_pivot[:], in0=sum_h[:, :, 0], scalar1=-1.0 / CH, scalar2=None, op0=ALU.mult
                 )
                 nc.vector.scalar_tensor_tensor(
-                    out=sums[:, :, 0], in0=negs[:], scalar=float(CH), in1=sums[:, :, 0], op0=ALU.mult, op1=ALU.add
+                    out=sum_h[:, :, 0],
+                    in0=neg_pivot[:],
+                    scalar=float(CH),
+                    in1=sum_h[:, :, 0],
+                    op0=ALU.mult,
+                    op1=ALU.add,
                 )
                 for j in range(NJ):
-                    pending.append((0, j, CH))
+                    for_scalar.append((0, j, CH))
 
-            def squares():
-                for c, j, width in pending[squared[0] :]:
-                    junk = stage.tile([P, 2 * CH], F32, name="junk", tag="junk", bufs=4)
+            def scalar_squares():
+                for c, j, rows in for_scalar[squared[0] :]:
+                    waste = stage.tile([P, 2 * CH], F32, name="waste", tag="waste", bufs=2)
                     nc.scalar.activation(
-                        out=junk[:, 0:width],
-                        in_=h_at(c, j, 0, width),
+                        out=waste[:, 0:rows],
+                        in_=h_at(c, j, 0, rows),
                         func=ACT.Square,
-                        bias=(negs[:, j : j + 1] if c == 0 else 0.0),
-                        accum_out=sqs[:, j, n_sq[j] : n_sq[j] + 1],
+                        bias=(neg_pivot[:, j : j + 1] if c == 0 else 0.0),
+                        accum_out=sum_sq[:, j, sq_used[j] : sq_used[j] + 1],
                     )
-                    n_sq[j] += 1
-                squared[0] = len(pending)
+                    sq_used[j] += 1
+                squared[0] = len(for_scalar)
 
-            wn3 = wn[:].rearrange("p (t n) -> p t n", t=4)
+            w3 = w_rows[:].rearrange("p (t n) -> p t n", t=4)
             for u in range(2):
-                nc.vector.memset(wn3[:, 2 * u : 2 * u + 2, 0 : 256 * u + BLK], 0.0)
-            nc.vector.memset(warm[:], 1.0)
-            nc.vector.memset(sqs[:], 0.0)
-            nc.vector.memset(gsum[:], 0.0)
+                nc.vector.memset(w3[:, 2 * u : 2 * u + 2, 0 : HALF * u + BLK], 0.0)
+            nc.vector.memset(one[:], 1.0)
+            nc.vector.memset(sum_sq[:], 0.0)
+            nc.vector.memset(sum_sq_g[:], 0.0)
+            nc.vector.memset(sum_sq_v[:], 0.0)
 
             b_src = breezeBiasWeights.rearrange("(u p e) n -> p u e n", u=2, e=2)
             t_src = treeWeights.rearrange("(u p e) n -> p u e n", u=2, e=2)
             for u in range(2):
-                c0 = 256 * u + BLK
-                nc.sync.dma_start(out=wn3[:, 2 * u : 2 * u + 2, c0:K], in_=b_src[:, u, :, c0:K])
-                nc.scalar.dma_start(out=tw[:, u, :, :], in_=t_src[:, u, :, 256 * u : 256 * u + 256])
+                c0 = HALF * u + BLK
+                nc.sync.dma_start(out=w3[:, 2 * u : 2 * u + 2, c0:K], in_=b_src[:, u, :, c0:K])
+                nc.scalar.dma_start(out=t_raw[:, u, :, :], in_=t_src[:, u, :, HALF * u : HALF * (u + 1)])
             for c in range(AHEAD):
                 load_x(c)
-                load_c(c)
+                load_init(c)
 
             make_identity(nc, ident[:])
-            nc.scalar.activation(out=warm2[:], in_=warm[:], func=ACT.Sqrt)
+            nc.scalar.activation(out=unused[:], in_=one[:], func=ACT.Sqrt)
 
             for u in range(2):
                 for q in range(2, 4):
-                    c0 = 256 * u + BLK
-                    nc.vector.memset(wn3[32 * q : 32 * q + 32, 2 * u : 2 * u + 2, c0 : c0 + BLK * (q - 1)], 0.0)
+                    c0 = HALF * u + BLK
+                    nc.vector.memset(w3[32 * q : 32 * q + 32, 2 * u : 2 * u + 2, c0 : c0 + BLK * (q - 1)], 0.0)
             for u in range(2):
                 for q in range(4):
                     rows = slice(32 * q, 32 * q + 32)
                     nc.vector.tensor_tensor(
-                        out=wn3[rows, 2 * u : 2 * u + 2, 256 * u + BLK * q : 256 * u + BLK * q + BLK],
-                        in0=tw[rows, u, :, BLK * q : BLK * q + BLK],
-                        in1=tw[rows, u, :, BLK * q : BLK * q + BLK],
+                        out=w3[rows, 2 * u : 2 * u + 2, HALF * u + BLK * q : HALF * u + BLK * (q + 1)],
+                        in0=t_raw[rows, u, :, BLK * q : BLK * (q + 1)],
+                        in1=t_raw[rows, u, :, BLK * q : BLK * (q + 1)],
                         op=ALU.mult,
                     )
-            w_src = wn[:].rearrange("p (t u i e) -> p u e i t", t=4, u=2, e=2)
+            w_src = w_rows[:].rearrange("p (t u i e) -> p u e i t", t=4, u=2, e=2)
             for j in range(NJ):
                 u, e = divmod(j, 2)
                 nc.vector.tensor_copy(
-                    out=wg[:, j * K : (j + 1) * K].rearrange("p (i t) -> p i t", t=4), in_=w_src[:, u, e]
+                    out=w_grouped[:, j * K : (j + 1) * K].rearrange("p (i t) -> p i t", t=4), in_=w_src[:, u, e]
                 )
-            nc.vector.quantize_mx(out=wc[:].bitcast(FP8X4), scales=ws[:], in_=wg[:])
+            nc.vector.quantize_mx(out=w_words[:].bitcast(FP8X4), scales=w_scales[:], in_=w_grouped[:])
 
-            transposes_x(0)
-            evac_x(0, 0, False)
-            evac_x(0, 1, False)
-            transposes_c(0)
-            evac_c(0, 0, False)
-            evac_c(0, 1, False)
-            quantise(0)
+            transpose_x(0)
+            empty_x_bank(0, 0, False)
+            empty_x_bank(0, 1, False)
+            transpose_init(0)
+            empty_init_bank(0, 0)
+            empty_init_bank(0, 1)
+            quantise_x(0)
+            transpose_x(1)
+            empty_x_bank(1, 0, False)
+            empty_x_bank(1, 1, False)
             for j in range(NJ):
-                mx(0, j, 1)
-            transposes_x(1)
-            evac_x(1, 0, False)
-            evac_x(1, 1, False)
-            transposes_c(1)
-            evac_c(1, 0, False)
-            evac_c(1, 1, False)
+                multiply(0, j)
+            transpose_init(1)
+            empty_init_bank(1, 0)
+            empty_init_bank(1, 1)
             for j in range(NJ):
                 add_init(0, j)
-            pivot()
-            quantise(1)
-            transposes_x(2)
-            transposes_c(2)
-            evac_x(2, 0, False)
-            evac_c(2, 0, False)
+            set_pivot()
+            quantise_x(1)
+            transpose_x(2)
+            transpose_init(2)
+            empty_x_bank(2, 0, False)
+            empty_init_bank(2, 0)
             for j in range(NJ):
-                mx(1, j, 1)
-            evac_x(2, 1, True)
-            evac_c(2, 1, True)
-            transposes_x(3)
-            quantise(2)
-            squares()
+                multiply(1, j)
+            empty_x_bank(2, 1, True)
+            empty_init_bank(2, 1)
+            transpose_x(3)
+            quantise_x(2)
+            scalar_squares()
 
             for i in range(1, NCH):
-                n2 = i + 2
-                if n2 < NCH:
-                    transposes_c(n2)
+                if i + 2 < NCH:
+                    transpose_init(i + 2)
                 add_init(i, 0)
                 add_init(i, 1)
                 if i + 1 < NCH:
-                    mx(i + 1, 0, 1)
-                    mx(i + 1, 1, 1 + REPEAT)
-                if n2 < NCH:
-                    evac_x(n2, 0, False)
-                    evac_x(n2, 1, True)
-                if n2 + 1 < NCH:
-                    transposes_x(n2 + 1)
-                squares()
+                    multiply(i + 1, 0)
+                    multiply(i + 1, 1)
+                if i + 2 < NCH:
+                    empty_x_bank(i + 2, 0, False)
+                    empty_x_bank(i + 2, 1, (i + 2) % VECTOR_EVERY == 0)
+                if i + 3 < NCH:
+                    transpose_x(i + 3)
+                scalar_squares()
                 add_init(i, 2)
                 add_init(i, 3)
                 if i + 1 < NCH:
-                    mx(i + 1, 2, 1)
-                    mx(i + 1, 3, 1 + REPEAT)
-                if n2 < NCH:
-                    evac_c(n2, 0, False)
-                    evac_c(n2, 1, False)
-                    quantise(n2)
+                    multiply(i + 1, 2)
+                    multiply(i + 1, 3)
+                if i + 2 < NCH:
+                    empty_init_bank(i + 2, 0)
+                    empty_init_bank(i + 2, 1)
+                    quantise_x(i + 2)
                 else:
-                    squares()
+                    scalar_squares()
 
-            nc.vector.tensor_reduce(out=gsum[:, 0:1], in_=gacc[:], axis=AX.X, op=ALU.add)
+            for c, j in VECTOR_PIECES:
+                nc.vector.scalar_tensor_tensor(
+                    out=v_square[:],
+                    in0=h_at(c, j, 0, CH),
+                    scalar=1.0,
+                    in1=h_at(c, j, 0, CH),
+                    op0=ALU.mult,
+                    op1=ALU.mult,
+                    accum_out=sum_sq_v[:, j : j + 1],
+                )
+            for j in sorted(g_running):
+                nc.vector.tensor_reduce(out=sum_sq_g[:, j : j + 1], in_=g_running[j][:], axis=AX.X, op=ALU.add)
 
-        nc.vector.tensor_reduce(out=s1[:], in_=sums[:], axis=AX.X, op=ALU.add)
-        nc.vector.tensor_scalar(out=dm[:], in0=s1[:], scalar1=1.0 / M, scalar2=None, op0=ALU.mult)
-        nc.vector.tensor_tensor(out=d2[:], in0=dm[:], in1=dm[:], op=ALU.mult)
-        nc.vector.scalar_tensor_tensor(out=d2[:], in0=gsum[:], scalar=-1.0 / M, in1=d2[:], op0=ALU.mult, op1=ALU.add)
-        nc.vector.tensor_reduce(out=s2[:], in_=sqs[:], axis=AX.X, op=ALU.add)
+        nc.vector.tensor_reduce(out=total_h[:], in_=sum_h[:], axis=AX.X, op=ALU.add)
+        nc.vector.tensor_scalar(out=mean[:], in0=total_h[:], scalar1=1.0 / M, scalar2=None, op0=ALU.mult)
+        nc.vector.tensor_tensor(out=less[:], in0=mean[:], in1=mean[:], op=ALU.mult)
         nc.vector.scalar_tensor_tensor(
-            out=var[:], in0=s2[:], scalar=1.0 / M, in1=d2[:], op0=ALU.mult, op1=ALU.subtract
+            out=less[:], in0=sum_sq_g[:], scalar=-1.0 / M, in1=less[:], op0=ALU.mult, op1=ALU.add
         )
-        nc.vector.tensor_scalar_max(out=var[:], in0=var[:], scalar1=1e-30)
+        nc.vector.scalar_tensor_tensor(
+            out=less[:], in0=sum_sq_v[:], scalar=-1.0 / M, in1=less[:], op0=ALU.mult, op1=ALU.add
+        )
+        nc.vector.tensor_reduce(out=total_sq[:], in_=sum_sq[:], axis=AX.X, op=ALU.add)
+        nc.vector.scalar_tensor_tensor(
+            out=var[:], in0=total_sq[:], scalar=1.0 / M, in1=less[:], op0=ALU.mult, op1=ALU.subtract
+        )
+        nc.vector.tensor_scalar_max(out=var[:], in0=var[:], scalar1=TINY)
         nc.scalar.activation(out=std[:], in_=var[:], func=ACT.Sqrt)
-        nc.scalar.activation(out=warm2[:], in_=warm[:], func=ACT.Sigmoid)
+        nc.scalar.activation(out=unused[:], in_=one[:], func=ACT.Sigmoid)
         nc.vector.tensor_scalar_add(out=std[:], in0=std[:], scalar1=EPS)
-        nc.vector.reciprocal(out=inv[:], in_=std[:])
+        nc.vector.reciprocal(out=scale[:], in_=std[:])
         nc.vector.scalar_tensor_tensor(
-            out=nb[:], in0=dm[:], scalar=-1.0, in1=inv[:], op0=ALU.mult, op1=ALU.mult
+            out=bias[:], in0=mean[:], scalar=-1.0, in1=scale[:], op0=ALU.mult, op1=ALU.mult
         )
-        nc.vector.tensor_tensor(out=nb0[:], in0=negs[:], in1=inv[:], op=ALU.mult)
-        nc.vector.tensor_tensor(out=nb0[:], in0=nb0[:], in1=nb[:], op=ALU.add)
 
         with ExitStack() as ph2:
             outp = ph2.enter_context(tc.tile_pool(name="outp", bufs=1))
@@ -344,35 +375,35 @@ def tile_treelayer_t_kernel(tc, x, x_init, treeWeights, breezeBiasWeights, out):
                 nc.vector.tensor_scalar(
                     out=h_at(c, j, lo, hi),
                     in0=h_at(c, j, lo, hi),
-                    scalar1=inv[:, j : j + 1],
-                    scalar2=(nb0 if c == 0 else nb)[:, j : j + 1],
+                    scalar1=scale[:, j : j + 1],
+                    scalar2=(bias0 if c == 0 else bias)[:, j : j + 1],
                     op0=ALU.mult,
                     op1=ALU.add,
                 )
 
             order = list(range(1, NCH)) + [0]
-            for k, c in enumerate(order + order):
+            for c in order:
                 cuts = [0, P, CH] if c == order[0] else [0, CH]
                 for lo, hi in zip(cuts[:-1], cuts[1:]):
                     for j in range(NJ):
-                        if k < NCH:
-                            normalise(c, j, lo, hi)
-                ost = outp.tile([P, TL, K], F32, name="ost", tag="ost", bufs=4)
+                        normalise(c, j, lo, hi)
+                if c == order[0]:
+                    nc.vector.tensor_tensor(out=bias0[:], in0=neg_pivot[:], in1=scale[:], op=ALU.mult)
+                    nc.vector.tensor_tensor(out=bias0[:], in0=bias0[:], in1=bias[:], op=ALU.add)
+                result = outp.tile([P, TL, K], F32, name="result", tag="result", bufs=4)
                 for tl in range(TL):
-                    tr = psum2.tile([P, K], F32, name="tr", tag="tr", bufs=8)
+                    bank = psum2.tile([P, K], F32, name="out_bank", tag="out_bank", bufs=8)
                     for j in range(NJ):
-                        nc.tensor.transpose(
-                            tr[:, j * P : (j + 1) * P], h_at(c, j, tl * P, (tl + 1) * P), ident[:]
-                        )
+                        nc.tensor.transpose(bank[:, j * P : (j + 1) * P], h_at(c, j, tl * P, (tl + 1) * P), ident[:])
                     nc.scalar.activation(
-                        out=ost[:, tl, :].rearrange("p (u i e) -> p u i e", u=2, e=2),
-                        in_=tr[:].rearrange("p (u e i) -> p u i e", u=2, e=2),
+                        out=result[:, tl, :].rearrange("p (u i e) -> p u i e", u=2, e=2),
+                        in_=bank[:].rearrange("p (u e i) -> p u i e", u=2, e=2),
                         func=ACT.Sigmoid,
                     )
                     if c == order[-1] and tl >= 1:
                         lo = 0 if tl == 1 else tl
                         nc.sync.dma_start(
-                            out=out_rows[:, c * TL + lo : c * TL + tl + 1, :], in_=ost[:, lo : tl + 1, :]
+                            out=out_rows[:, c * TL + lo : c * TL + tl + 1, :], in_=result[:, lo : tl + 1, :]
                         )
                 if c != order[-1]:
-                    nc.sync.dma_start(out=out_rows[:, c * TL : (c + 1) * TL, :], in_=ost[:])
+                    nc.sync.dma_start(out=out_rows[:, c * TL : (c + 1) * TL, :], in_=result[:])

@@ -28,11 +28,11 @@ AHEAD = 4
 
 FLOPS = 2 * 2 * M * K * K
 
-GPSIMD_PIECES = [(c, 0) for c in range(1, NCH)] + [(1, 1), (3, 1)]
+GPSIMD_PIECES = [(c, 0) for c in range(1, NCH)] + [(1, 1), (3, 1), (5, 1), (7, 1)]
 VECTOR_PIECES = [(NCH - 1, 2)]
 PAIR_FIRST = list(range(1, 12, 2))
 SQ_COLS = 10
-VECTOR_EVERY = 4
+VECTOR_EVERY = 2
 
 
 def tile_treelayer_t_kernel(tc, x, x_init, treeWeights, breezeBiasWeights, out):

from contextlib import ExitStack

import concourse.mybir as mybir
from concourse.masks import make_identity

F32 = mybir.dt.float32
BF16 = mybir.dt.bfloat16
U32 = mybir.dt.uint32
U8 = mybir.dt.uint8
FP8X4 = mybir.dt.float8_e4m3fn_x4
ALU = mybir.AluOpType
ACT = mybir.ActivationFunctionType
AX = mybir.AxisListType

P = 128
M = 8192
K = 512
BLK = 64
HALF = K // 2
EPS = 1e-6
TINY = 1e-30
ROWS_PER_PARTITION = M // P
TL = 4
CH = TL * P
NCH = M // CH
NJ = K // P
AHEAD = 4

FLOPS = 2 * 2 * M * K * K

GPSIMD_PIECES = [(c, 0) for c in range(1, NCH)] + [(1, 1), (3, 1), (5, 1), (7, 1)]
VECTOR_PIECES = [(NCH - 1, 2)]
PAIR_FIRST = list(range(1, 12, 2))
SQ_COLS = 10
VECTOR_EVERY = 2


def tile_treelayer_t_kernel(tc, x, x_init, treeWeights, breezeBiasWeights, out):
    nc = tc.nc
    x_rows = x.rearrange("(p t) k -> p (t k)", t=ROWS_PER_PARTITION)
    init_rows = x_init.rearrange("(p t) n -> p (t n)", t=ROWS_PER_PARTITION)
    out_rows = out.rearrange("(p t) n -> p t n", t=ROWS_PER_PARTITION)

    with ExitStack() as ctx:
        ctx.enter_context(tc.manual_schedule())
        keep = ctx.enter_context(tc.tile_pool(name="keep", bufs=1))

        ident = keep.tile([P, P], F32, name="ident")
        w_words = keep.tile([P, K], U32, name="w_words", align_bytes=64)
        w_scales = keep.tile([P, K], U8, name="w_scales", align_bytes=64)
        sum_h = keep.tile([P, NJ, NCH], F32, name="sum_h")
        sum_sq = keep.tile([P, NJ, SQ_COLS], F32, name="sum_sq")
        sum_sq_g = keep.tile([P, NJ], F32, name="sum_sq_g")
        sum_sq_v = keep.tile([P, NJ], F32, name="sum_sq_v")
        neg_pivot = keep.tile([P, NJ], F32, name="neg_pivot")
        one = keep.tile([P, 1], F32, name="one")
        unused = keep.tile([P, 1], F32, name="unused")
        total_h = keep.tile([P, NJ], F32, name="total_h")
        total_sq = keep.tile([P, NJ], F32, name="total_sq")
        mean = keep.tile([P, NJ], F32, name="mean")
        less = keep.tile([P, NJ], F32, name="less")
        var = keep.tile([P, NJ], F32, name="var")
        std = keep.tile([P, NJ], F32, name="std")
        scale = keep.tile([P, NJ], F32, name="scale")
        bias = keep.tile([P, NJ], F32, name="bias")
        bias0 = keep.tile([P, NJ], F32, name="bias0")

        h_home = {}
        for first, count in [(0, 1)] + [(c, 2) for c in range(1, NCH - 1, 2)] + [(NCH - 1, 1)]:
            h_tile = keep.tile([P, NJ, count * CH], F32, name="h%d" % first)
            for c in range(first, first + count):
                h_home[c] = (h_tile, (c - first) * CH)

        def h_at(c, j, lo, hi):
            h_tile, off = h_home[c]
            return h_tile[:, j, off + lo : off + hi]

        with ExitStack() as ph1:
            stage = ph1.enter_context(tc.tile_pool(name="stage", bufs=1))
            psum = ph1.enter_context(tc.psum_pool(name="psum", bufs=1))

            t_raw = stage.tile([P, 2, 2, HALF], BF16, name="t_raw")
            w_rows = stage.tile([P, 4 * K], BF16, name="w_rows")
            w_grouped = stage.tile([P, 4 * K], BF16, name="w_grouped", align_bytes=64)
            g_square = stage.tile([P, CH], F32, name="g_square")
            v_square = stage.tile([P, CH], F32, name="v_square")

            x_nat = {}
            init_nat = {}
            x_banks = {}
            init_banks = {}
            x_grouped = {}
            init_t = {}
            x_words = {}
            x_scales = {}
            product = {}
            g_running = {}
            for_scalar = []
            squared = [0]
            sq_used = [0] * NJ

            def load_x(c):
                x_nat_t = stage.tile([P, TL * K], BF16, name="x_nat", tag="x_nat", bufs=AHEAD)
                nc.sync.dma_start(out=x_nat_t[:], in_=x_rows[:, c * TL * K : (c + 1) * TL * K])
                x_nat[c] = x_nat_t

            def load_init(c):
                init_nat_t = stage.tile([P, TL * K], BF16, name="init_nat", tag="init_nat", bufs=AHEAD)
                nc.sync.dma_start(out=init_nat_t[:], in_=init_rows[:, c * TL * K : (c + 1) * TL * K])
                init_nat[c] = init_nat_t

            def transpose_x(c):
                words = x_nat[c][:].bitcast(F32)
                for b in range(2):
                    bank = psum.tile([P, CH], F32, name="x_bank", tag="x_bank", bufs=2)
                    for r in range(2):
                        for u in range(2):
                            src = (2 * b + r) * HALF + u * P
                            dst = u * HALF + r * P
                            nc.tensor.transpose(bank[:, dst : dst + P], words[:, src : src + P], ident[:])
                    x_banks[c, b] = bank
                x_grouped_t = stage.tile([P, 4 * CH], BF16, name="x_grouped", tag="x_grouped", bufs=3, align_bytes=64)
                x_grouped[c] = x_grouped_t
                if c + AHEAD < NCH:
                    load_x(c + AHEAD)

            def transpose_init(c):
                words = init_nat[c][:].bitcast(F32)
                for u in range(2):
                    bank = psum.tile([P, CH], F32, name="init_bank", tag="init_bank", bufs=2)
                    for tl in range(TL):
                        src = tl * HALF + u * P
                        nc.tensor.transpose(bank[:, tl * P : (tl + 1) * P], words[:, src : src + P], ident[:])
                    init_banks[c, u] = bank
                init_t_t = stage.tile([P, 2 * CH], F32, name="init_t", tag="init_t", bufs=3)
                init_t[c] = init_t_t
                if c + AHEAD < NCH:
                    load_init(c + AHEAD)

            def copy_out(on_vector, dst, src):
                if on_vector:
                    nc.vector.tensor_copy(out=dst, in_=src)
                else:
                    nc.scalar.copy(out=dst, in_=src)

            def empty_x_bank(c, b, on_vector):
                dst = x_grouped[c][:].bitcast(F32)[:, b * CH : (b + 1) * CH].rearrange("p (m u) -> p m u", u=2)
                src = x_banks[c, b][:].rearrange("p (u m) -> p m u", u=2)
                copy_out(on_vector, dst, src)

            def empty_init_bank(c, u):
                copy_out(False, init_t[c][:, u * CH : (u + 1) * CH], init_banks[c, u][:])

            def quantise_x(c):
                words = stage.tile([P, CH], U32, name="x_words", tag="x_words", bufs=3, align_bytes=64)
                scales = stage.tile([P, CH], U8, name="x_scales", tag="x_scales", bufs=3, align_bytes=64)
                nc.vector.quantize_mx(out=words[:].bitcast(FP8X4), scales=scales[:], in_=x_grouped[c][:])
                x_words[c] = words
                x_scales[c] = scales

            def multiply(c, j):
                acc = psum.tile([P, CH], F32, name="acc", tag="acc", bufs=4)
                nc.tensor.matmul_mx(
                    out=acc[:],
                    lhsT=w_words[:, j * P : (j + 1) * P].bitcast(FP8X4),
                    lhsT_scale=w_scales[:, j * P : (j + 1) * P],
                    rhs=x_words[c][:].bitcast(FP8X4),
                    rhs_scale=x_scales[c][:],
                    start=True,
                    stop=True,
                )
                product[c, j] = acc

            def on_scalar(c, j):
                return (c, j) not in GPSIMD_PIECES and (c, j) not in VECTOR_PIECES

            def add_init(c, j):
                u, e = divmod(j, 2)
                init_view = init_t[c][:].bitcast(BF16).rearrange("p (u m e) -> p u m e", u=2, e=2)[:, u, :, e]
                nc.vector.scalar_tensor_tensor(
                    out=h_at(c, j, 0, CH),
                    in0=product[c, j][:],
                    scalar=(0.0 if c == 0 else neg_pivot[:, j : j + 1]),
                    in1=init_view,
                    op0=ALU.add,
                    op1=ALU.add,
                    accum_out=sum_h[:, j, c : c + 1],
                )
                if (c, j) in GPSIMD_PIECES:
                    first = j not in g_running
                    if first:
                        running = stage.tile([P, CH], F32, name="g_running%d" % j)
                        g_running[j] = running
                    nc.gpsimd.tensor_tensor(
                        out=(g_running[j] if first else g_square)[:],
                        in0=h_at(c, j, 0, CH),
                        in1=h_at(c, j, 0, CH),
                        op=ALU.mult,
                    )
                    if not first:
                        nc.gpsimd.tensor_tensor(out=g_running[j][:], in0=g_running[j][:], in1=g_square[:], op=ALU.add)
                elif c > 0 and on_scalar(c, j):
                    if c - 1 in PAIR_FIRST and on_scalar(c - 1, j):
                        for_scalar.append((c - 1, j, 2 * CH))
                    elif not (c in PAIR_FIRST and on_scalar(c + 1, j)):
                        for_scalar.append((c, j, CH))

            def set_pivot():
                nc.vector.tensor_scalar(
                    out=neg_pivot[:], in0=sum_h[:, :, 0], scalar1=-1.0 / CH, scalar2=None, op0=ALU.mult
                )
                nc.vector.scalar_tensor_tensor(
                    out=sum_h[:, :, 0],
                    in0=neg_pivot[:],
                    scalar=float(CH),
                    in1=sum_h[:, :, 0],
                    op0=ALU.mult,
                    op1=ALU.add,
                )
                for j in range(NJ):
                    for_scalar.append((0, j, CH))

            def scalar_squares():
                for c, j, rows in for_scalar[squared[0] :]:
                    waste = stage.tile([P, 2 * CH], F32, name="waste", tag="waste", bufs=2)
                    nc.scalar.activation(
                        out=waste[:, 0:rows],
                        in_=h_at(c, j, 0, rows),
                        func=ACT.Square,
                        bias=(neg_pivot[:, j : j + 1] if c == 0 else 0.0),
                        accum_out=sum_sq[:, j, sq_used[j] : sq_used[j] + 1],
                    )
                    sq_used[j] += 1
                squared[0] = len(for_scalar)

            w3 = w_rows[:].rearrange("p (t n) -> p t n", t=4)
            for u in range(2):
                nc.vector.memset(w3[:, 2 * u : 2 * u + 2, 0 : HALF * u + BLK], 0.0)
            nc.vector.memset(one[:], 1.0)
            nc.vector.memset(sum_sq[:], 0.0)
            nc.vector.memset(sum_sq_g[:], 0.0)
            nc.vector.memset(sum_sq_v[:], 0.0)

            b_src = breezeBiasWeights.rearrange("(u p e) n -> p u e n", u=2, e=2)
            t_src = treeWeights.rearrange("(u p e) n -> p u e n", u=2, e=2)
            for u in range(2):
                c0 = HALF * u + BLK
                nc.sync.dma_start(out=w3[:, 2 * u : 2 * u + 2, c0:K], in_=b_src[:, u, :, c0:K])
                nc.scalar.dma_start(out=t_raw[:, u, :, :], in_=t_src[:, u, :, HALF * u : HALF * (u + 1)])
            for c in range(AHEAD):
                load_x(c)
                load_init(c)

            make_identity(nc, ident[:])
            nc.scalar.activation(out=unused[:], in_=one[:], func=ACT.Sqrt)

            for u in range(2):
                for q in range(2, 4):
                    c0 = HALF * u + BLK
                    nc.vector.memset(w3[32 * q : 32 * q + 32, 2 * u : 2 * u + 2, c0 : c0 + BLK * (q - 1)], 0.0)
            for u in range(2):
                for q in range(4):
                    rows = slice(32 * q, 32 * q + 32)
                    nc.vector.tensor_tensor(
                        out=w3[rows, 2 * u : 2 * u + 2, HALF * u + BLK * q : HALF * u + BLK * (q + 1)],
                        in0=t_raw[rows, u, :, BLK * q : BLK * (q + 1)],
                        in1=t_raw[rows, u, :, BLK * q : BLK * (q + 1)],
                        op=ALU.mult,
                    )
            w_src = w_rows[:].rearrange("p (t u i e) -> p u e i t", t=4, u=2, e=2)
            for j in range(NJ):
                u, e = divmod(j, 2)
                nc.vector.tensor_copy(
                    out=w_grouped[:, j * K : (j + 1) * K].rearrange("p (i t) -> p i t", t=4), in_=w_src[:, u, e]
                )
            nc.vector.quantize_mx(out=w_words[:].bitcast(FP8X4), scales=w_scales[:], in_=w_grouped[:])

            transpose_x(0)
            empty_x_bank(0, 0, False)
            empty_x_bank(0, 1, False)
            transpose_init(0)
            empty_init_bank(0, 0)
            empty_init_bank(0, 1)
            quantise_x(0)
            transpose_x(1)
            empty_x_bank(1, 0, False)
            empty_x_bank(1, 1, False)
            for j in range(NJ):
                multiply(0, j)
            transpose_init(1)
            empty_init_bank(1, 0)
            empty_init_bank(1, 1)
            for j in range(NJ):
                add_init(0, j)
            set_pivot()
            quantise_x(1)
            transpose_x(2)
            transpose_init(2)
            empty_x_bank(2, 0, False)
            empty_init_bank(2, 0)
            for j in range(NJ):
                multiply(1, j)
            empty_x_bank(2, 1, True)
            empty_init_bank(2, 1)
            transpose_x(3)
            quantise_x(2)
            scalar_squares()

            for i in range(1, NCH):
                if i + 2 < NCH:
                    transpose_init(i + 2)
                add_init(i, 0)
                add_init(i, 1)
                if i + 1 < NCH:
                    multiply(i + 1, 0)
                    multiply(i + 1, 1)
                if i + 2 < NCH:
                    empty_x_bank(i + 2, 0, False)
                    empty_x_bank(i + 2, 1, (i + 2) % VECTOR_EVERY == 0)
                if i + 3 < NCH:
                    transpose_x(i + 3)
                scalar_squares()
                add_init(i, 2)
                add_init(i, 3)
                if i + 1 < NCH:
                    multiply(i + 1, 2)
                    multiply(i + 1, 3)
                if i + 2 < NCH:
                    empty_init_bank(i + 2, 0)
                    empty_init_bank(i + 2, 1)
                    quantise_x(i + 2)
                else:
                    scalar_squares()

            for c, j in VECTOR_PIECES:
                nc.vector.scalar_tensor_tensor(
                    out=v_square[:],
                    in0=h_at(c, j, 0, CH),
                    scalar=1.0,
                    in1=h_at(c, j, 0, CH),
                    op0=ALU.mult,
                    op1=ALU.mult,
                    accum_out=sum_sq_v[:, j : j + 1],
                )
            for j in sorted(g_running):
                nc.vector.tensor_reduce(out=sum_sq_g[:, j : j + 1], in_=g_running[j][:], axis=AX.X, op=ALU.add)

        nc.vector.tensor_reduce(out=total_h[:], in_=sum_h[:], axis=AX.X, op=ALU.add)
        nc.vector.tensor_scalar(out=mean[:], in0=total_h[:], scalar1=1.0 / M, scalar2=None, op0=ALU.mult)
        nc.vector.tensor_tensor(out=less[:], in0=mean[:], in1=mean[:], op=ALU.mult)
        nc.vector.scalar_tensor_tensor(
            out=less[:], in0=sum_sq_g[:], scalar=-1.0 / M, in1=less[:], op0=ALU.mult, op1=ALU.add
        )
        nc.vector.scalar_tensor_tensor(
            out=less[:], in0=sum_sq_v[:], scalar=-1.0 / M, in1=less[:], op0=ALU.mult, op1=ALU.add
        )
        nc.vector.tensor_reduce(out=total_sq[:], in_=sum_sq[:], axis=AX.X, op=ALU.add)
        nc.vector.scalar_tensor_tensor(
            out=var[:], in0=total_sq[:], scalar=1.0 / M, in1=less[:], op0=ALU.mult, op1=ALU.subtract
        )
        nc.vector.tensor_scalar_max(out=var[:], in0=var[:], scalar1=TINY)
        nc.scalar.activation(out=std[:], in_=var[:], func=ACT.Sqrt)
        nc.scalar.activation(out=unused[:], in_=one[:], func=ACT.Sigmoid)
        nc.vector.tensor_scalar_add(out=std[:], in0=std[:], scalar1=EPS)
        nc.vector.reciprocal(out=scale[:], in_=std[:])
        nc.vector.scalar_tensor_tensor(
            out=bias[:], in0=mean[:], scalar=-1.0, in1=scale[:], op0=ALU.mult, op1=ALU.mult
        )

        with ExitStack() as ph2:
            outp = ph2.enter_context(tc.tile_pool(name="outp", bufs=1))
            psum2 = ph2.enter_context(tc.psum_pool(name="psum2", bufs=1))

            def normalise(c, j, lo, hi):
                nc.vector.tensor_scalar(
                    out=h_at(c, j, lo, hi),
                    in0=h_at(c, j, lo, hi),
                    scalar1=scale[:, j : j + 1],
                    scalar2=(bias0 if c == 0 else bias)[:, j : j + 1],
                    op0=ALU.mult,
                    op1=ALU.add,
                )

            order = list(range(1, NCH)) + [0]
            for c in order:
                cuts = [0, P, CH] if c == order[0] else [0, CH]
                for lo, hi in zip(cuts[:-1], cuts[1:]):
                    for j in range(NJ):
                        normalise(c, j, lo, hi)
                if c == order[0]:
                    nc.vector.tensor_tensor(out=bias0[:], in0=neg_pivot[:], in1=scale[:], op=ALU.mult)
                    nc.vector.tensor_tensor(out=bias0[:], in0=bias0[:], in1=bias[:], op=ALU.add)
                result = outp.tile([P, TL, K], F32, name="result", tag="result", bufs=4)
                for tl in range(TL):
                    bank = psum2.tile([P, K], F32, name="out_bank", tag="out_bank", bufs=8)
                    for j in range(NJ):
                        nc.tensor.transpose(bank[:, j * P : (j + 1) * P], h_at(c, j, tl * P, (tl + 1) * P), ident[:])
                    nc.scalar.activation(
                        out=result[:, tl, :].rearrange("p (u i e) -> p u i e", u=2, e=2),
                        in_=bank[:].rearrange("p (u e i) -> p u i e", u=2, e=2),
                        func=ACT.Sigmoid,
                    )
                    if c == order[-1] and tl >= 1:
                        lo = 0 if tl == 1 else tl
                        nc.sync.dma_start(
                            out=out_rows[:, c * TL + lo : c * TL + tl + 1, :], in_=result[:, lo : tl + 1, :]
                        )
                if c != order[-1]:
                    nc.sync.dma_start(out=out_rows[:, c * TL : (c + 1) * TL, :], in_=result[:])
